import numpy as np
import ml_dtypes


def mxq(x, axis, fmt="e4m3"):
    dtype, down = {"e4m3": (ml_dtypes.float8_e4m3fn, 7), "e5m2": (ml_dtypes.float8_e5m2, 14)}[fmt]
    v = np.moveaxis(np.asarray(x, np.float32).astype(ml_dtypes.bfloat16).astype(np.float64), axis, -1)
    blocks = v.reshape(v.shape[:-1] + (-1, 32))
    amax = np.abs(blocks).max(-1, keepdims=True)
    byte = np.maximum(np.where(amax > 0, np.frexp(amax)[1] - 1 + 127, 0) - down, 1)
    scale = np.exp2(byte - 127.0)
    codes = (blocks / scale).astype(np.float32).astype(dtype).astype(np.float64)
    return np.moveaxis((codes * scale).reshape(v.shape), -1, axis)


WIDE = False


def mx_kscale(k):
    if not WIDE:
        return np.ones(k)
    levels = np.array([10, -10, 5, -5, 0])
    a = np.random.permutation(np.resize(levels, k // 512 * 4)).reshape(k // 512, 4)
    idx = np.arange(k)
    return np.exp2(a[idx // 512, idx % 128 // 32])


BF16 = ml_dtypes.bfloat16


def bf(x):
    return np.asarray(x, np.float32).astype(BF16)


def f64(x):
    return np.asarray(x).astype(np.float64)


E2M1 = np.array([0.0, 0.5, 1.0, 1.5, 2.0, 3.0, 4.0, 6.0, -0.0, -0.5, -1.0, -1.5, -2.0, -3.0, -4.0, -6.0])


def pack_weight(w, fmt):
    k, n = w.shape
    w = f64(bf(w)).reshape(k // 32, 32, n)
    amax = np.abs(w).max(1)
    if fmt == "e4m3":
        byte = np.frexp(amax)[1] - 1 + 127 - 7
    else:
        mant, ex = np.frexp(amax / 6.0)
        byte = np.where(mant > 0.5, ex, ex - 1) + 127
    byte = np.clip(np.where(amax > 0, byte, 1), 1, 254)
    scaled = (w * np.exp2(127.0 - byte)[:, None, :]).reshape(k, n).astype(np.float32)
    by_word = np.ascontiguousarray(scaled.reshape(k // 512, 128, 4, n).transpose(0, 1, 3, 2))
    if fmt == "e4m3":
        words = by_word.astype(ml_dtypes.float8_e4m3fn).view(np.uint8)
    else:
        c = by_word.astype(ml_dtypes.float4_e2m1fn).view(np.uint8) & 0xF
        words = c[..., 0::2] | (c[..., 1::2] << 4)
    return np.ascontiguousarray(words), np.ascontiguousarray(byte.astype(np.uint8).reshape(k // 512, 16, n))


def unpack_weight(words, scales, fmt):
    g, p, n, _ = words.shape
    if fmt == "e4m3":
        vals = np.ascontiguousarray(words).view(ml_dtypes.float8_e4m3fn).astype(np.float64)
    else:
        nib = np.empty((g, p, n, 4), np.uint8)
        nib[..., 0::2] = words & 0xF
        nib[..., 1::2] = words >> 4
        vals = E2M1[nib]
    vals = vals * np.repeat(np.exp2(scales.astype(np.float64) - 127.0), 8, axis=1)[..., None]
    return vals.transpose(0, 1, 3, 2).reshape(g * 512, n)


B, C_IN, H, W, D, P, NC = 16, 512, 16, 16, 512, 2048, 256
HW = H * W


def sigmoid(v):
    return 1.0 / (1.0 + np.exp(-v))


def setup_inputs():
    s = mx_kscale(D)
    h_relu = bf(np.maximum(np.random.standard_normal((B, D, H, W)) * np.sqrt(2.0), 0.0) * s[None, :, None, None])
    conv2_w = np.random.standard_normal((D, D)) * np.sqrt(2.0 / D) / s[None, :]
    words, scales = pack_weight(np.ascontiguousarray(conv2_w.T), "e4m3")
    conv2_b = bf(np.random.standard_normal(D) * 0.5)
    prototypes = bf(np.random.uniform(size=(P, D)))
    return {"h_relu": h_relu,
            "conv2_w_words": words,
            "conv2_w_scales": scales,
            "conv2_b": conv2_b,
            "prototypes": prototypes}


def reference(h_relu, conv2_w_words, conv2_w_scales, conv2_b, prototypes):
    h = f64(h_relu).reshape(B, D, HW)
    z = (unpack_weight(conv2_w_words, conv2_w_scales, "e4m3").T @ mxq(h, 1, "e4m3")) + f64(conv2_b)[None, :, None]
    f = sigmoid(z)
    pr = f64(prototypes)
    f2 = np.sum(f * f, axis=1)
    p2 = np.sum(pr * pr, axis=1)
    fp = mxq(pr, 1, "e4m3") @ mxq(f, 1, "e4m3")
    distances = f2[:, None, :] + p2[None, :, None] - 2.0 * fp
    return np.min(distances, axis=-1)

@@ -1,0 +1,316 @@
+from contextlib import ExitStack
+
+import concourse.mybir as mybir
+from concourse.masks import make_identity
+
+BF16 = mybir.dt.bfloat16
+F32 = mybir.dt.float32
+I32 = mybir.dt.int32
+U32 = mybir.dt.uint32
+U8 = mybir.dt.uint8
+FP8X4 = mybir.dt.float8_e4m3fn_x4
+ALU = mybir.AluOpType
+ACT = mybir.ActivationFunctionType
+AXIS = mybir.AxisListType
+
+P = 128
+PACK = 4
+BANK = 512
+
+IMAGES = 16
+CHANNELS = 512
+POSITIONS = 256
+PROTOS = 2048
+
+GROUP_IMAGES = 4
+RUN = P // GROUP_IMAGES
+GROUPS = IMAGES // GROUP_IMAGES
+TILES_PER_CHUNK = BANK // P
+CHUNKS = IMAGES * POSITIONS // BANK
+CHUNKS_PER_GROUP = CHUNKS // GROUPS
+PROTO_TILES = PROTOS // P
+PROTO_CHUNKS = PROTOS // BANK
+NORMS_PER_CHUNK = PROTO_TILES // CHUNKS
+
+FLOPS = 2 * IMAGES * POSITIONS * CHANNELS * (CHANNELS + PROTOS)
+
+
+def tile_protopnet_pa_kernel(tc, h_relu, conv2_w_words, conv2_w_scales, conv2_b, prototypes, out):
+    nc = tc.nc
+    with ExitStack() as ctx:
+        keep = ctx.enter_context(tc.tile_pool(name="keep", bufs=1))
+        stage = ctx.enter_context(tc.tile_pool(name="stage", bufs=2))
+        conv_psum = ctx.enter_context(tc.psum_pool(name="conv_psum", bufs=2))
+        flip_psum = ctx.enter_context(tc.psum_pool(name="flip_psum", bufs=2))
+        dist_psum = ctx.enter_context(tc.psum_pool(name="dist_psum", bufs=4))
+        ctx.enter_context(tc.manual_schedule())
+
+        h_raw = keep.tile([P, IMAGES, PACK, POSITIONS], BF16)
+        p_raw = keep.tile([P, PROTO_TILES, CHANNELS], BF16)
+        w_codes = keep.tile([P, CHANNELS], U32, align_bytes=64)
+        w_scales = keep.tile([P, CHANNELS], U8, align_bytes=64)
+        h_codes = keep.tile([P, CHUNKS, BANK], U32, align_bytes=64)
+        h_scales = keep.tile([P, CHUNKS, BANK], U8, align_bytes=64)
+        p_codes = keep.tile([P, PROTO_CHUNKS, BANK], U32, align_bytes=64)
+        p_scales = keep.tile([P, PROTO_CHUNKS, BANK], U8, align_bytes=64)
+        ident_f32 = keep.tile([P, P], F32)
+        ident_bf16 = keep.tile([P, P], BF16)
+        bias_rows = keep.tile([P, P], BF16)
+        bias = keep.tile([P, PACK], F32)
+        p2 = keep.tile([P, PROTO_TILES], F32)
+        best = keep.tile([P, IMAGES, PROTO_TILES], F32)
+        result = keep.tile([P, IMAGES, PROTO_TILES], F32)
+        result_rows = keep.tile([P, 2, P], F32)
+        table_warmer = keep.tile([P, 1], F32)
+
+        nc.vector.memset(w_scales[:].bitcast(I32), 0)
+        nc.vector.memset(bias_rows[:], 0.0)
+        nc.vector.memset(table_warmer[:], 0.0)
+        nc.scalar.activation(out=table_warmer[:], in_=table_warmer[:], func=ACT.Sigmoid)
+        make_identity(nc, ident_bf16[:])
+        make_identity(nc, ident_f32[:])
+
+        scale_rows = conv2_w_scales.rearrange("g q n -> (g q) n")
+        for quadrant in range(4):
+            nc.sync.dma_start(
+                out=w_scales[32 * quadrant : 32 * quadrant + 4, :].bitcast(I32),
+                in_=scale_rows[4 * quadrant : 4 * quadrant + 4, :].bitcast(I32),
+            )
+        nc.sync.dma_start(
+            out=w_codes[:].bitcast(I32), in_=conv2_w_words.rearrange("g p n t -> (g p) (n t)").bitcast(I32)
+        )
+        nc.scalar.dma_start(out=bias_rows[0:PACK, :], in_=conv2_b.rearrange("(t m) -> t m", m=P))
+        h_view = h_relu.rearrange("b (p t) y x -> p b t (y x)", t=PACK)
+        p_view = prototypes.rearrange("(k r) d -> r k d", r=P)
+
+        def load_group(g):
+            images = slice(g * GROUP_IMAGES, (g + 1) * GROUP_IMAGES)
+            nc.sync.dma_start(out=h_raw[:, images], in_=h_view[:, images])
+
+        load_group(0)
+        for c in range(PROTO_CHUNKS):
+            tiles = slice(c * TILES_PER_CHUNK, (c + 1) * TILES_PER_CHUNK)
+            nc.sync.dma_start(out=p_raw[:, tiles, :], in_=p_view[:, tiles, :])
+        for g in range(1, GROUPS):
+            load_group(g)
+
+        bias_flipped = flip_psum.tile([P, P], BF16, tag="flip")
+        nc.tensor.transpose(out=bias_flipped[:], in_=bias_rows[:], identity=ident_bf16[:])
+        nc.vector.tensor_copy(out=bias[:], in_=bias_flipped[:, 0:PACK])
+
+        h_grouped_of = {}
+        feat_of = {}
+        f_grouped_of = {}
+        f_codes_of = {}
+        f_scales_of = {}
+        neg_half_f2_of = {}
+        f2_of = {}
+        running_max_of = {}
+
+        def regroup(engine, dst, src):
+            engine.tensor_scalar(out=dst, in0=src, scalar1=1.0, scalar2=0.0, op0=ALU.mult, op1=ALU.add)
+
+        def group_h(q, engine):
+            h_grouped = stage.tile([P, BANK, PACK], BF16, align_bytes=64)
+            h_grouped_of[q] = h_grouped
+            g = q // CHUNKS_PER_GROUP
+            images = slice(g * GROUP_IMAGES, (g + 1) * GROUP_IMAGES)
+            for j in range(TILES_PER_CHUNK):
+                tile_in_group = (q % CHUNKS_PER_GROUP) * TILES_PER_CHUNK + j
+                run = slice(tile_in_group * RUN, (tile_in_group + 1) * RUN)
+                regroup(
+                    engine,
+                    h_grouped[:, j * P : (j + 1) * P, :].rearrange("p (b r) t -> p b r t", r=RUN),
+                    h_raw[:, images, :, run].rearrange("p b t r -> p b r t"),
+                )
+
+        def quantise_h(q):
+            nc.vector.quantize_mx(
+                out=h_codes[:, q, :].bitcast(FP8X4),
+                scales=h_scales[:, q, :],
+                in_=h_grouped_of[q][:].rearrange("p c t -> p (c t)"),
+            )
+
+        def prepare_prototypes(c):
+            p_grouped = stage.tile([P, BANK, PACK], BF16, align_bytes=64)
+            for i in range(TILES_PER_CHUNK):
+                k = c * TILES_PER_CHUNK + i
+                flipped = flip_psum.tile([P, PACK, P], BF16, tag="flip")
+                for t in range(PACK):
+                    nc.tensor.transpose(
+                        out=flipped[:, t, :], in_=p_raw[:, k, t * P : (t + 1) * P], identity=ident_bf16[:]
+                    )
+                dst = p_grouped[:, i * P : (i + 1) * P, :]
+                src = flipped[:].rearrange("p t r -> p r t")
+                if i % 2 == 0:
+                    nc.vector.tensor_copy(out=dst, in_=src)
+                else:
+                    nc.scalar.copy(out=dst, in_=src)
+            nc.vector.quantize_mx(
+                out=p_codes[:, c, :].bitcast(FP8X4),
+                scales=p_scales[:, c, :],
+                in_=p_grouped[:].rearrange("p c t -> p (c t)"),
+            )
+
+        def prototype_norm(k):
+            squares = stage.tile([P, CHANNELS], BF16, tag="squares")
+            nc.scalar.activation(out=squares[:], in_=p_raw[:, k, :], func=ACT.Square, accum_out=p2[:, k : k + 1])
+
+        def conv(q):
+            feat = stage.tile([P, PACK, BANK], F32)
+            feat_of[q] = feat
+            for t in range(PACK):
+                z = conv_psum.tile([P, BANK], F32)
+                nc.tensor.matmul_mx(
+                    out=z[:],
+                    lhsT=w_codes[:, t * P : (t + 1) * P].bitcast(FP8X4),
+                    lhsT_scale=w_scales[:, t * P : (t + 1) * P],
+                    rhs=h_codes[:, q, :].bitcast(FP8X4),
+                    rhs_scale=h_scales[:, q, :],
+                    start=True,
+                    stop=True,
+                )
+                nc.scalar.activation(out=feat[:, t, :], in_=z[:], func=ACT.Sigmoid, bias=bias[:, t : t + 1], scale=1.0)
+
+        def group_f(q):
+            f_grouped = stage.tile([P, BANK, PACK], BF16, align_bytes=64)
+            f_grouped_of[q] = f_grouped
+            regroup(nc.gpsimd, f_grouped[:], feat_of[q][:].rearrange("p t c -> p c t"))
+
+        def quantise_f(q):
+            f_codes = stage.tile([P, BANK], U32, align_bytes=64)
+            f_scales = stage.tile([P, BANK], U8, align_bytes=64)
+            f_codes_of[q] = f_codes
+            f_scales_of[q] = f_scales
+            nc.vector.quantize_mx(
+                out=f_codes[:].bitcast(FP8X4),
+                scales=f_scales[:],
+                in_=f_grouped_of[q][:].rearrange("p c t -> p (c t)"),
+            )
+
+        def feature_norms(q, tiles):
+            if q not in f2_of:
+                f2 = stage.tile([P, TILES_PER_CHUNK], F32)
+                f2_of[q] = f2
+            for j in tiles:
+                flipped = flip_psum.tile([P, PACK, P], F32, tag="flip")
+                for t in range(PACK):
+                    nc.tensor.transpose(
+                        out=flipped[:, t, :], in_=feat_of[q][:, t, j * P : (j + 1) * P], identity=ident_f32[:]
+                    )
+                squares = stage.tile([P, CHANNELS], BF16, tag="squares")
+                nc.scalar.activation(
+                    out=squares[:],
+                    in_=flipped[:].rearrange("p t d -> p (t d)"),
+                    func=ACT.Square,
+                    accum_out=f2_of[q][:, j : j + 1],
+                )
+
+        def halve_norms(q):
+            neg_half_f2 = stage.tile([P, TILES_PER_CHUNK], F32)
+            neg_half_f2_of[q] = neg_half_f2
+            nc.scalar.mul(out=neg_half_f2[:], in_=f2_of[q][:], mul=-0.5)
+
+        def distances(q, j):
+            g = q // CHUNKS_PER_GROUP
+            first_of_group = q % CHUNKS_PER_GROUP == 0 and j == 0
+            if first_of_group:
+                running_max = stage.tile([P, PROTOS], F32)
+                running_max_of[g] = running_max
+            shift = neg_half_f2_of[q][:, j : j + 1]
+            for c in range(PROTO_CHUNKS):
+                fp = dist_psum.tile([P, BANK], F32, tag="dist")
+                nc.tensor.matmul_mx(
+                    out=fp[:],
+                    lhsT=f_codes_of[q][:, j * P : (j + 1) * P].bitcast(FP8X4),
+                    lhsT_scale=f_scales_of[q][:, j * P : (j + 1) * P],
+                    rhs=p_codes[:, c, :].bitcast(FP8X4),
+                    rhs_scale=p_scales[:, c, :],
+                    start=True,
+                    stop=True,
+                )
+                kept = running_max_of[g][:, c * BANK : (c + 1) * BANK]
+                if first_of_group:
+                    nc.scalar.activation(out=kept, in_=fp[:], func=ACT.Identity, bias=shift, scale=1.0)
+                else:
+                    nc.vector.scalar_tensor_tensor(
+                        out=kept, in0=fp[:], scalar=shift, in1=kept, op0=ALU.add, op1=ALU.max
+                    )
+
+        def fold_group(g):
+            images = slice(g * GROUP_IMAGES, (g + 1) * GROUP_IMAGES)
+            for c in range(PROTO_CHUNKS):
+                flipped = dist_psum.tile([P, TILES_PER_CHUNK, P], F32, tag="dist")
+                for i in range(TILES_PER_CHUNK):
+                    k = c * TILES_PER_CHUNK + i
+                    nc.tensor.transpose(
+                        out=flipped[:, i, :], in_=running_max_of[g][:, k * P : (k + 1) * P], identity=ident_f32[:]
+                    )
+                tiles = slice(c * TILES_PER_CHUNK, (c + 1) * TILES_PER_CHUNK)
+                nc.vector.tensor_reduce(
+                    out=best[:, images, tiles].rearrange("p b k -> p k b"),
+                    in_=flipped[:].rearrange("p k (b r) -> p k b r", r=RUN),
+                    op=ALU.max,
+                    axis=AXIS.X,
+                )
+
+        group_h(0, nc.vector)
+        quantise_h(0)
+        group_h(1, nc.gpsimd)
+        prepare_prototypes(0)
+        conv(0)
+        prepare_prototypes(1)
+        prepare_prototypes(2)
+        quantise_h(1)
+        group_f(0)
+        feature_norms(0, range(TILES_PER_CHUNK))
+        halve_norms(0)
+        prepare_prototypes(3)
+        quantise_f(0)
+
+        for q in range(CHUNKS):
+            distances(q, 0)
+            if q + 2 < CHUNKS:
+                group_h(q + 2, nc.gpsimd)
+            if q + 1 < CHUNKS:
+                conv(q + 1)
+            if q > 0 and q % CHUNKS_PER_GROUP == 0:
+                fold_group(q // CHUNKS_PER_GROUP - 1)
+            if q + 1 < CHUNKS:
+                group_f(q + 1)
+            distances(q, 1)
+            if q + 1 < CHUNKS:
+                feature_norms(q + 1, range(0, 2))
+            distances(q, 2)
+            if q + 1 < CHUNKS:
+                feature_norms(q + 1, range(2, 4))
+                halve_norms(q + 1)
+                quantise_f(q + 1)
+            distances(q, 3)
+            if q + 2 < CHUNKS:
+                quantise_h(q + 2)
+            for k in range(q * NORMS_PER_CHUNK, (q + 1) * NORMS_PER_CHUNK):
+                prototype_norm(k)
+        fold_group(GROUPS - 1)
+
+        nc.vector.scalar_tensor_tensor(
+            out=result[:],
+            in0=best[:],
+            scalar=-2.0,
+            in1=p2[:].unsqueeze(1).to_broadcast([P, IMAGES, PROTO_TILES]),
+            op0=ALU.mult,
+            op1=ALU.add,
+        )
+        half = IMAGES // 2
+        rows = dist_psum.tile([P, 2, P], F32, tag="dist")
+        for s in range(2):
+            nc.tensor.transpose(
+                out=rows[:, s, :],
+                in_=result[:, s * half : (s + 1) * half, :].rearrange("p b k -> p (b k)"),
+                identity=ident_f32[:],
+            )
+        nc.vector.tensor_copy(out=result_rows[:], in_=rows[:])
+        for s in range(2):
+            nc.sync.dma_start(
+                out=out[s * half : (s + 1) * half, :].rearrange("b (k r) -> (b k) r", r=P), in_=result_rows[:, s, :]
+            )

@@ -40,9 +40,8 @@ def tile_protopnet_pa_kernel(tc, h_relu, conv2_w_words, conv2_w_scales, conv2_b,
     with ExitStack() as ctx:
         keep = ctx.enter_context(tc.tile_pool(name="keep", bufs=1))
         stage = ctx.enter_context(tc.tile_pool(name="stage", bufs=2))
-        conv_psum = ctx.enter_context(tc.psum_pool(name="conv_psum", bufs=2))
-        flip_psum = ctx.enter_context(tc.psum_pool(name="flip_psum", bufs=2))
-        dist_psum = ctx.enter_context(tc.psum_pool(name="dist_psum", bufs=4))
+        scalar_psum = ctx.enter_context(tc.psum_pool(name="scalar_psum", bufs=4))
+        vector_psum = ctx.enter_context(tc.psum_pool(name="vector_psum", bufs=4))
         ctx.enter_context(tc.manual_schedule())
 
         h_raw = keep.tile([P, IMAGES, PACK, POSITIONS], BF16)
@@ -94,7 +93,7 @@ def tile_protopnet_pa_kernel(tc, h_relu, conv2_w_words, conv2_w_scales, conv2_b,
         for g in range(1, GROUPS):
             load_group(g)
 
-        bias_flipped = flip_psum.tile([P, P], BF16, tag="flip")
+        bias_flipped = vector_psum.tile([P, P], BF16, tag="v")
         nc.tensor.transpose(out=bias_flipped[:], in_=bias_rows[:], identity=ident_bf16[:])
         nc.vector.tensor_copy(out=bias[:], in_=bias_flipped[:, 0:PACK])
 
@@ -135,7 +134,7 @@ def tile_protopnet_pa_kernel(tc, h_relu, conv2_w_words, conv2_w_scales, conv2_b,
             p_grouped = stage.tile([P, BANK, PACK], BF16, align_bytes=64)
             for i in range(TILES_PER_CHUNK):
                 k = c * TILES_PER_CHUNK + i
-                flipped = flip_psum.tile([P, PACK, P], BF16, tag="flip")
+                flipped = vector_psum.tile([P, PACK, P], BF16, tag="v")
                 for t in range(PACK):
                     nc.tensor.transpose(
                         out=flipped[:, t, :], in_=p_raw[:, k, t * P : (t + 1) * P], identity=ident_bf16[:]
@@ -160,7 +159,7 @@ def tile_protopnet_pa_kernel(tc, h_relu, conv2_w_words, conv2_w_scales, conv2_b,
             feat = stage.tile([P, PACK, BANK], F32)
             feat_of[q] = feat
             for t in range(PACK):
-                z = conv_psum.tile([P, BANK], F32)
+                z = scalar_psum.tile([P, BANK], F32, tag="s")
                 nc.tensor.matmul_mx(
                     out=z[:],
                     lhsT=w_codes[:, t * P : (t + 1) * P].bitcast(FP8X4),
@@ -193,7 +192,7 @@ def tile_protopnet_pa_kernel(tc, h_relu, conv2_w_words, conv2_w_scales, conv2_b,
                 f2 = stage.tile([P, TILES_PER_CHUNK], F32)
                 f2_of[q] = f2
             for j in tiles:
-                flipped = flip_psum.tile([P, PACK, P], F32, tag="flip")
+                flipped = scalar_psum.tile([P, PACK, P], F32, tag="s")
                 for t in range(PACK):
                     nc.tensor.transpose(
                         out=flipped[:, t, :], in_=feat_of[q][:, t, j * P : (j + 1) * P], identity=ident_f32[:]
@@ -219,7 +218,10 @@ def tile_protopnet_pa_kernel(tc, h_relu, conv2_w_words, conv2_w_scales, conv2_b,
                 running_max_of[g] = running_max
             shift = neg_half_f2_of[q][:, j : j + 1]
             for c in range(PROTO_CHUNKS):
-                fp = dist_psum.tile([P, BANK], F32, tag="dist")
+                if first_of_group:
+                    fp = scalar_psum.tile([P, BANK], F32, tag="s")
+                else:
+                    fp = vector_psum.tile([P, BANK], F32, tag="v")
                 nc.tensor.matmul_mx(
                     out=fp[:],
                     lhsT=f_codes_of[q][:, j * P : (j + 1) * P].bitcast(FP8X4),
@@ -240,7 +242,7 @@ def tile_protopnet_pa_kernel(tc, h_relu, conv2_w_words, conv2_w_scales, conv2_b,
         def fold_group(g):
             images = slice(g * GROUP_IMAGES, (g + 1) * GROUP_IMAGES)
             for c in range(PROTO_CHUNKS):
-                flipped = dist_psum.tile([P, TILES_PER_CHUNK, P], F32, tag="dist")
+                flipped = vector_psum.tile([P, TILES_PER_CHUNK, P], F32, tag="v")
                 for i in range(TILES_PER_CHUNK):
                     k = c * TILES_PER_CHUNK + i
                     nc.tensor.transpose(
@@ -256,37 +258,36 @@ def tile_protopnet_pa_kernel(tc, h_relu, conv2_w_words, conv2_w_scales, conv2_b,
 
         group_h(0, nc.vector)
         quantise_h(0)
-        group_h(1, nc.gpsimd)
         prepare_prototypes(0)
         conv(0)
+        group_h(1, nc.gpsimd)
         prepare_prototypes(1)
         prepare_prototypes(2)
-        quantise_h(1)
         group_f(0)
         feature_norms(0, range(TILES_PER_CHUNK))
         halve_norms(0)
-        prepare_prototypes(3)
         quantise_f(0)
+        prepare_prototypes(3)
+        quantise_h(1)
 
         for q in range(CHUNKS):
+            if q > 0 and q % CHUNKS_PER_GROUP == 0:
+                fold_group(q // CHUNKS_PER_GROUP - 1)
             distances(q, 0)
             if q + 2 < CHUNKS:
                 group_h(q + 2, nc.gpsimd)
-            if q + 1 < CHUNKS:
-                conv(q + 1)
-            if q > 0 and q % CHUNKS_PER_GROUP == 0:
-                fold_group(q // CHUNKS_PER_GROUP - 1)
-            if q + 1 < CHUNKS:
-                group_f(q + 1)
             distances(q, 1)
             if q + 1 < CHUNKS:
-                feature_norms(q + 1, range(0, 2))
+                conv(q + 1)
+                group_f(q + 1)
             distances(q, 2)
+            if q + 1 < CHUNKS:
+                feature_norms(q + 1, range(0, 2))
+            distances(q, 3)
             if q + 1 < CHUNKS:
                 feature_norms(q + 1, range(2, 4))
                 halve_norms(q + 1)
                 quantise_f(q + 1)
-            distances(q, 3)
             if q + 2 < CHUNKS:
                 quantise_h(q + 2)
             for k in range(q * NORMS_PER_CHUNK, (q + 1) * NORMS_PER_CHUNK):
@@ -302,7 +303,7 @@ def tile_protopnet_pa_kernel(tc, h_relu, conv2_w_words, conv2_w_scales, conv2_b,
             op1=ALU.add,
         )
         half = IMAGES // 2
-        rows = dist_psum.tile([P, 2, P], F32, tag="dist")
+        rows = vector_psum.tile([P, 2, P], F32, tag="v")
         for s in range(2):
             nc.tensor.transpose(
                 out=rows[:, s, :],

@@ -42,7 +42,6 @@ def tile_protopnet_pa_kernel(tc, h_relu, conv2_w_words, conv2_w_scales, conv2_b,
         stage = ctx.enter_context(tc.tile_pool(name="stage", bufs=2))
         scalar_psum = ctx.enter_context(tc.psum_pool(name="scalar_psum", bufs=4))
         vector_psum = ctx.enter_context(tc.psum_pool(name="vector_psum", bufs=4))
-        ctx.enter_context(tc.manual_schedule())
 
         h_raw = keep.tile([P, IMAGES, PACK, POSITIONS], BF16)
         p_raw = keep.tile([P, PROTO_TILES, CHANNELS], BF16)
@@ -69,6 +68,14 @@ def tile_protopnet_pa_kernel(tc, h_relu, conv2_w_words, conv2_w_scales, conv2_b,
         make_identity(nc, ident_bf16[:])
         make_identity(nc, ident_f32[:])
 
+        h_view = h_relu.rearrange("b (p t) y x -> p b t (y x)", t=PACK)
+        p_view = prototypes.rearrange("(k r) d -> r k d", r=P)
+
+        def load_group(g):
+            images = slice(g * GROUP_IMAGES, (g + 1) * GROUP_IMAGES)
+            nc.sync.dma_start(out=h_raw[:, images], in_=h_view[:, images])
+
+        load_group(0)
         scale_rows = conv2_w_scales.rearrange("g q n -> (g q) n")
         for quadrant in range(4):
             nc.sync.dma_start(
@@ -79,14 +86,6 @@ def tile_protopnet_pa_kernel(tc, h_relu, conv2_w_words, conv2_w_scales, conv2_b,
             out=w_codes[:].bitcast(I32), in_=conv2_w_words.rearrange("g p n t -> (g p) (n t)").bitcast(I32)
         )
         nc.scalar.dma_start(out=bias_rows[0:PACK, :], in_=conv2_b.rearrange("(t m) -> t m", m=P))
-        h_view = h_relu.rearrange("b (p t) y x -> p b t (y x)", t=PACK)
-        p_view = prototypes.rearrange("(k r) d -> r k d", r=P)
-
-        def load_group(g):
-            images = slice(g * GROUP_IMAGES, (g + 1) * GROUP_IMAGES)
-            nc.sync.dma_start(out=h_raw[:, images], in_=h_view[:, images])
-
-        load_group(0)
         for c in range(PROTO_CHUNKS):
             tiles = slice(c * TILES_PER_CHUNK, (c + 1) * TILES_PER_CHUNK)
             nc.sync.dma_start(out=p_raw[:, tiles, :], in_=p_view[:, tiles, :])
@@ -102,9 +101,8 @@ def tile_protopnet_pa_kernel(tc, h_relu, conv2_w_words, conv2_w_scales, conv2_b,
         f_grouped_of = {}
         f_codes_of = {}
         f_scales_of = {}
-        neg_half_f2_of = {}
         f2_of = {}
-        running_max_of = {}
+        running_min_of = {}
 
         def regroup(engine, dst, src):
             engine.tensor_scalar(out=dst, in0=src, scalar1=1.0, scalar2=0.0, op0=ALU.mult, op1=ALU.add)
@@ -142,9 +140,9 @@ def tile_protopnet_pa_kernel(tc, h_relu, conv2_w_words, conv2_w_scales, conv2_b,
                 dst = p_grouped[:, i * P : (i + 1) * P, :]
                 src = flipped[:].rearrange("p t r -> p r t")
                 if i % 2 == 0:
-                    nc.vector.tensor_copy(out=dst, in_=src)
+                    nc.vector.tensor_scalar_mul(out=dst, in0=src, scalar1=-2.0)
                 else:
-                    nc.scalar.copy(out=dst, in_=src)
+                    nc.scalar.mul(out=dst, in_=src, mul=-2.0)
             nc.vector.quantize_mx(
                 out=p_codes[:, c, :].bitcast(FP8X4),
                 scales=p_scales[:, c, :],
@@ -205,18 +203,13 @@ def tile_protopnet_pa_kernel(tc, h_relu, conv2_w_words, conv2_w_scales, conv2_b,
                     accum_out=f2_of[q][:, j : j + 1],
                 )
 
-        def halve_norms(q):
-            neg_half_f2 = stage.tile([P, TILES_PER_CHUNK], F32)
-            neg_half_f2_of[q] = neg_half_f2
-            nc.scalar.mul(out=neg_half_f2[:], in_=f2_of[q][:], mul=-0.5)
-
         def distances(q, j):
             g = q // CHUNKS_PER_GROUP
             first_of_group = q % CHUNKS_PER_GROUP == 0 and j == 0
             if first_of_group:
-                running_max = stage.tile([P, PROTOS], F32)
-                running_max_of[g] = running_max
-            shift = neg_half_f2_of[q][:, j : j + 1]
+                running_min = stage.tile([P, PROTOS], F32)
+                running_min_of[g] = running_min
+            f2_column = f2_of[q][:, j : j + 1]
             for c in range(PROTO_CHUNKS):
                 if first_of_group:
                     fp = scalar_psum.tile([P, BANK], F32, tag="s")
@@ -231,12 +224,12 @@ def tile_protopnet_pa_kernel(tc, h_relu, conv2_w_words, conv2_w_scales, conv2_b,
                     start=True,
                     stop=True,
                 )
-                kept = running_max_of[g][:, c * BANK : (c + 1) * BANK]
+                kept = running_min_of[g][:, c * BANK : (c + 1) * BANK]
                 if first_of_group:
-                    nc.scalar.activation(out=kept, in_=fp[:], func=ACT.Identity, bias=shift, scale=1.0)
+                    nc.scalar.activation(out=kept, in_=fp[:], func=ACT.Identity, bias=f2_column, scale=1.0)
                 else:
                     nc.vector.scalar_tensor_tensor(
-                        out=kept, in0=fp[:], scalar=shift, in1=kept, op0=ALU.add, op1=ALU.max
+                        out=kept, in0=fp[:], scalar=f2_column, in1=kept, op0=ALU.add, op1=ALU.min
                     )
 
         def fold_group(g):
@@ -246,13 +239,13 @@ def tile_protopnet_pa_kernel(tc, h_relu, conv2_w_words, conv2_w_scales, conv2_b,
                 for i in range(TILES_PER_CHUNK):
                     k = c * TILES_PER_CHUNK + i
                     nc.tensor.transpose(
-                        out=flipped[:, i, :], in_=running_max_of[g][:, k * P : (k + 1) * P], identity=ident_f32[:]
+                        out=flipped[:, i, :], in_=running_min_of[g][:, k * P : (k + 1) * P], identity=ident_f32[:]
                     )
                 tiles = slice(c * TILES_PER_CHUNK, (c + 1) * TILES_PER_CHUNK)
                 nc.vector.tensor_reduce(
                     out=best[:, images, tiles].rearrange("p b k -> p k b"),
                     in_=flipped[:].rearrange("p k (b r) -> p k b r", r=RUN),
-                    op=ALU.max,
+                    op=ALU.min,
                     axis=AXIS.X,
                 )
 
@@ -265,7 +258,6 @@ def tile_protopnet_pa_kernel(tc, h_relu, conv2_w_words, conv2_w_scales, conv2_b,
         prepare_prototypes(2)
         group_f(0)
         feature_norms(0, range(TILES_PER_CHUNK))
-        halve_norms(0)
         quantise_f(0)
         prepare_prototypes(3)
         quantise_h(1)
@@ -286,7 +278,6 @@ def tile_protopnet_pa_kernel(tc, h_relu, conv2_w_words, conv2_w_scales, conv2_b,
             distances(q, 3)
             if q + 1 < CHUNKS:
                 feature_norms(q + 1, range(2, 4))
-                halve_norms(q + 1)
                 quantise_f(q + 1)
             if q + 2 < CHUNKS:
                 quantise_h(q + 2)
@@ -294,13 +285,8 @@ def tile_protopnet_pa_kernel(tc, h_relu, conv2_w_words, conv2_w_scales, conv2_b,
                 prototype_norm(k)
         fold_group(GROUPS - 1)
 
-        nc.vector.scalar_tensor_tensor(
-            out=result[:],
-            in0=best[:],
-            scalar=-2.0,
-            in1=p2[:].unsqueeze(1).to_broadcast([P, IMAGES, PROTO_TILES]),
-            op0=ALU.mult,
-            op1=ALU.add,
+        nc.vector.tensor_tensor(
+            out=result[:], in0=best[:], in1=p2[:].unsqueeze(1).to_broadcast([P, IMAGES, PROTO_TILES]), op=ALU.add
         )
         half = IMAGES // 2
         rows = vector_psum.tile([P, 2, P], F32, tag="v")

@@ -42,6 +42,7 @@ def tile_protopnet_pa_kernel(tc, h_relu, conv2_w_words, conv2_w_scales, conv2_b,
         stage = ctx.enter_context(tc.tile_pool(name="stage", bufs=2))
         scalar_psum = ctx.enter_context(tc.psum_pool(name="scalar_psum", bufs=4))
         vector_psum = ctx.enter_context(tc.psum_pool(name="vector_psum", bufs=4))
+        ctx.enter_context(tc.manual_schedule())
 
         h_raw = keep.tile([P, IMAGES, PACK, POSITIONS], BF16)
         p_raw = keep.tile([P, PROTO_TILES, CHANNELS], BF16)
@@ -108,7 +109,7 @@ def tile_protopnet_pa_kernel(tc, h_relu, conv2_w_words, conv2_w_scales, conv2_b,
             engine.tensor_scalar(out=dst, in0=src, scalar1=1.0, scalar2=0.0, op0=ALU.mult, op1=ALU.add)
 
         def group_h(q, engine):
-            h_grouped = stage.tile([P, BANK, PACK], BF16, align_bytes=64)
+            h_grouped = stage.tile([P, BANK, PACK], BF16, align_bytes=64, bufs=1)
             h_grouped_of[q] = h_grouped
             g = q // CHUNKS_PER_GROUP
             images = slice(g * GROUP_IMAGES, (g + 1) * GROUP_IMAGES)

@@ -15,7 +15,9 @@ AXIS = mybir.AxisListType
 
 P = 128
 PACK = 4
+PAIR = 2
 BANK = 512
+HALF = BANK // 2
 
 IMAGES = 16
 CHANNELS = 512
@@ -30,7 +32,8 @@ CHUNKS = IMAGES * POSITIONS // BANK
 CHUNKS_PER_GROUP = CHUNKS // GROUPS
 PROTO_TILES = PROTOS // P
 PROTO_CHUNKS = PROTOS // BANK
-NORMS_PER_CHUNK = PROTO_TILES // CHUNKS
+FLIPS = BANK // (PAIR * P)
+WARMUPS = 8
 
 FLOPS = 2 * IMAGES * POSITIONS * CHANNELS * (CHANNELS + PROTOS)
 
@@ -46,28 +49,29 @@ def tile_protopnet_pa_kernel(tc, h_relu, conv2_w_words, conv2_w_scales, conv2_b,
 
         h_raw = keep.tile([P, IMAGES, PACK, POSITIONS], BF16)
         p_raw = keep.tile([P, PROTO_TILES, CHANNELS], BF16)
+        w_codes_raw = keep.tile([P, CHANNELS], U32, align_bytes=64)
+        w_scales_raw = keep.tile([P, CHANNELS], U8, align_bytes=64)
         w_codes = keep.tile([P, CHANNELS], U32, align_bytes=64)
         w_scales = keep.tile([P, CHANNELS], U8, align_bytes=64)
         h_codes = keep.tile([P, CHUNKS, BANK], U32, align_bytes=64)
         h_scales = keep.tile([P, CHUNKS, BANK], U8, align_bytes=64)
         p_codes = keep.tile([P, PROTO_CHUNKS, BANK], U32, align_bytes=64)
         p_scales = keep.tile([P, PROTO_CHUNKS, BANK], U8, align_bytes=64)
-        ident_f32 = keep.tile([P, P], F32)
-        ident_bf16 = keep.tile([P, P], BF16)
-        bias_rows = keep.tile([P, P], BF16)
+        ident = keep.tile([P, P], F32)
+        bias_rows = keep.tile([P, P], F32)
         bias = keep.tile([P, PACK], F32)
         p2 = keep.tile([P, PROTO_TILES], F32)
         best = keep.tile([P, IMAGES, PROTO_TILES], F32)
         result = keep.tile([P, IMAGES, PROTO_TILES], F32)
-        result_rows = keep.tile([P, 2, P], F32)
         table_warmer = keep.tile([P, 1], F32)
+        zeros = keep.tile([P, BANK], BF16)
 
-        nc.vector.memset(w_scales[:].bitcast(I32), 0)
+        nc.vector.memset(w_scales_raw[:].bitcast(I32), 0)
+        nc.vector.memset(zeros[:], 0.0)
         nc.vector.memset(bias_rows[:], 0.0)
         nc.vector.memset(table_warmer[:], 0.0)
         nc.scalar.activation(out=table_warmer[:], in_=table_warmer[:], func=ACT.Sigmoid)
-        make_identity(nc, ident_bf16[:])
-        make_identity(nc, ident_f32[:])
+        make_identity(nc, ident[:])
 
         h_view = h_relu.rearrange("b (p t) y x -> p b t (y x)", t=PACK)
         p_view = prototypes.rearrange("(k r) d -> r k d", r=P)
@@ -76,28 +80,46 @@ def tile_protopnet_pa_kernel(tc, h_relu, conv2_w_words, conv2_w_scales, conv2_b,
             images = slice(g * GROUP_IMAGES, (g + 1) * GROUP_IMAGES)
             nc.sync.dma_start(out=h_raw[:, images], in_=h_view[:, images])
 
-        load_group(0)
         scale_rows = conv2_w_scales.rearrange("g q n -> (g q) n")
         for quadrant in range(4):
             nc.sync.dma_start(
-                out=w_scales[32 * quadrant : 32 * quadrant + 4, :].bitcast(I32),
+                out=w_scales_raw[32 * quadrant : 32 * quadrant + 4, :].bitcast(I32),
                 in_=scale_rows[4 * quadrant : 4 * quadrant + 4, :].bitcast(I32),
             )
         nc.sync.dma_start(
-            out=w_codes[:].bitcast(I32), in_=conv2_w_words.rearrange("g p n t -> (g p) (n t)").bitcast(I32)
+            out=w_codes_raw[:].bitcast(I32), in_=conv2_w_words.rearrange("g p n t -> (g p) (n t)").bitcast(I32)
         )
-        nc.scalar.dma_start(out=bias_rows[0:PACK, :], in_=conv2_b.rearrange("(t m) -> t m", m=P))
+        nc.scalar.dma_start(
+            out=bias_rows[0 : CHANNELS // (PAIR * P), :].bitcast(BF16),
+            in_=conv2_b.rearrange("(u i) -> u i", i=PAIR * P),
+        )
+        for b in range(GROUP_IMAGES):
+            nc.sync.dma_start(out=h_raw[:, b], in_=h_view[:, b])
         for c in range(PROTO_CHUNKS):
             tiles = slice(c * TILES_PER_CHUNK, (c + 1) * TILES_PER_CHUNK)
             nc.sync.dma_start(out=p_raw[:, tiles, :], in_=p_view[:, tiles, :])
         for g in range(1, GROUPS):
             load_group(g)
 
-        bias_flipped = vector_psum.tile([P, P], BF16, tag="v")
-        nc.tensor.transpose(out=bias_flipped[:], in_=bias_rows[:], identity=ident_bf16[:])
-        nc.vector.tensor_copy(out=bias[:], in_=bias_flipped[:, 0:PACK])
+        nc.vector.tensor_copy(
+            out=w_codes[:].bitcast(I32).rearrange("p (u e m) -> p u e m", u=2, e=PAIR),
+            in_=w_codes_raw[:].bitcast(I32).rearrange("p (u m e) -> p u e m", u=2, e=PAIR),
+        )
+        nc.vector.tensor_copy(
+            out=w_scales[:].rearrange("p (u e m) -> p u e m", u=2, e=PAIR),
+            in_=w_scales_raw[:].rearrange("p (u m e) -> p u e m", u=2, e=PAIR),
+        )
+
+        unread = scalar_psum.tile([P, BANK], F32, tag="s")
+        for i in range(WARMUPS):
+            nc.tensor.matmul(out=unread[:], lhsT=zeros[:, 0:P], rhs=zeros[:], start=True, stop=True)
+
+        bias_flipped = vector_psum.tile([P, P], F32, tag="v")
+        nc.tensor.transpose(out=bias_flipped[:], in_=bias_rows[:], identity=ident[:])
+        nc.vector.tensor_copy(out=bias[:], in_=bias_flipped[:, 0 : PACK // PAIR].bitcast(BF16))
 
         h_grouped_of = {}
+        p_grouped_of = {}
         feat_of = {}
         f_grouped_of = {}
         f_codes_of = {}
@@ -105,12 +127,21 @@ def tile_protopnet_pa_kernel(tc, h_relu, conv2_w_words, conv2_w_scales, conv2_b,
         f2_of = {}
         running_min_of = {}
 
-        def regroup(engine, dst, src):
-            engine.tensor_scalar(out=dst, in0=src, scalar1=1.0, scalar2=0.0, op0=ALU.mult, op1=ALU.add)
+        def regroup(engine, dst, src, factor=1.0):
+            engine.tensor_scalar(out=dst, in0=src, scalar1=factor, scalar2=0.0, op0=ALU.mult, op1=ALU.add)
 
-        def group_h(q, engine):
+        def new_h_grouped(q):
             h_grouped = stage.tile([P, BANK, PACK], BF16, align_bytes=64, bufs=1)
             h_grouped_of[q] = h_grouped
+
+        def group_first_h():
+            new_h_grouped(0)
+            by_image = h_grouped_of[0][:].rearrange("p (j b r) t -> p b j r t", b=GROUP_IMAGES, r=RUN)
+            for b in range(GROUP_IMAGES):
+                regroup(nc.vector, by_image[:, b], h_raw[:, b, :, 0:P].rearrange("p t (j r) -> p j r t", r=RUN))
+
+        def group_h(q, engine):
+            new_h_grouped(q)
             g = q // CHUNKS_PER_GROUP
             images = slice(g * GROUP_IMAGES, (g + 1) * GROUP_IMAGES)
             for j in range(TILES_PER_CHUNK):
@@ -118,7 +149,7 @@ def tile_protopnet_pa_kernel(tc, h_relu, conv2_w_words, conv2_w_scales, conv2_b,
                 run = slice(tile_in_group * RUN, (tile_in_group + 1) * RUN)
                 regroup(
                     engine,
-                    h_grouped[:, j * P : (j + 1) * P, :].rearrange("p (b r) t -> p b r t", r=RUN),
+                    h_grouped_of[q][:, j * P : (j + 1) * P, :].rearrange("p (b r) t -> p b r t", r=RUN),
                     h_raw[:, images, :, run].rearrange("p b t r -> p b r t"),
                 )
 
@@ -129,61 +160,92 @@ def tile_protopnet_pa_kernel(tc, h_relu, conv2_w_words, conv2_w_scales, conv2_b,
                 in_=h_grouped_of[q][:].rearrange("p c t -> p (c t)"),
             )
 
-        def prepare_prototypes(c):
-            p_grouped = stage.tile([P, BANK, PACK], BF16, align_bytes=64)
-            for i in range(TILES_PER_CHUNK):
-                k = c * TILES_PER_CHUNK + i
-                flipped = vector_psum.tile([P, PACK, P], BF16, tag="v")
-                for t in range(PACK):
-                    nc.tensor.transpose(
-                        out=flipped[:, t, :], in_=p_raw[:, k, t * P : (t + 1) * P], identity=ident_bf16[:]
-                    )
-                dst = p_grouped[:, i * P : (i + 1) * P, :]
-                src = flipped[:].rearrange("p t r -> p r t")
-                if i % 2 == 0:
-                    nc.vector.tensor_scalar_mul(out=dst, in0=src, scalar1=-2.0)
-                else:
-                    nc.scalar.mul(out=dst, in_=src, mul=-2.0)
+        def flip_prototypes(c, pair, on_scalar):
+            if c not in p_grouped_of:
+                p_grouped = stage.tile([P, BANK, PACK], BF16, align_bytes=64)
+                p_grouped_of[c] = p_grouped
+            if on_scalar:
+                flipped = scalar_psum.tile([P, FLIPS, 2, P], F32, tag="s")
+            else:
+                flipped = vector_psum.tile([P, FLIPS, 2, P], F32, tag="v")
+            for i in range(FLIPS):
+                k = c * TILES_PER_CHUNK + pair * FLIPS + i
+                words = p_raw[:, k, :].bitcast(F32)
+                for u in range(2):
+                    nc.tensor.transpose(out=flipped[:, i, u, :], in_=words[:, u * P : (u + 1) * P], identity=ident[:])
+            rows = p_grouped_of[c][:, pair * FLIPS * P : (pair + 1) * FLIPS * P, :]
+            dst = rows.rearrange("p r t -> p (r t)").bitcast(F32).rearrange("p (i r u) -> p i r u", u=2, r=P)
+            src = flipped[:].rearrange("p i u r -> p i r u")
+            if on_scalar:
+                nc.scalar.copy(out=dst, in_=src)
+            else:
+                nc.vector.tensor_copy(out=dst, in_=src)
+
+        def quantise_prototypes(c):
             nc.vector.quantize_mx(
                 out=p_codes[:, c, :].bitcast(FP8X4),
                 scales=p_scales[:, c, :],
-                in_=p_grouped[:].rearrange("p c t -> p (c t)"),
+                in_=p_grouped_of[c][:].rearrange("p c t -> p (c t)"),
             )
 
         def prototype_norm(k):
             squares = stage.tile([P, CHANNELS], BF16, tag="squares")
             nc.scalar.activation(out=squares[:], in_=p_raw[:, k, :], func=ACT.Square, accum_out=p2[:, k : k + 1])
 
+        def conv_pass(q, t, out_columns, columns):
+            nc.tensor.matmul_mx(
+                out=out_columns,
+                lhsT=w_codes[:, t * P : (t + 1) * P].bitcast(FP8X4),
+                lhsT_scale=w_scales[:, t * P : (t + 1) * P],
+                rhs=h_codes[:, q, columns].bitcast(FP8X4),
+                rhs_scale=h_scales[:, q, columns],
+                start=True,
+                stop=True,
+            )
+
+        def sigmoid(q, t, columns, z):
+            nc.scalar.activation(
+                out=feat_of[q][:, t, columns], in_=z, func=ACT.Sigmoid, bias=bias[:, t : t + 1], scale=1.0
+            )
+
         def conv(q):
             feat = stage.tile([P, PACK, BANK], F32)
             feat_of[q] = feat
             for t in range(PACK):
                 z = scalar_psum.tile([P, BANK], F32, tag="s")
-                nc.tensor.matmul_mx(
-                    out=z[:],
-                    lhsT=w_codes[:, t * P : (t + 1) * P].bitcast(FP8X4),
-                    lhsT_scale=w_scales[:, t * P : (t + 1) * P],
-                    rhs=h_codes[:, q, :].bitcast(FP8X4),
-                    rhs_scale=h_scales[:, q, :],
-                    start=True,
-                    stop=True,
-                )
-                nc.scalar.activation(out=feat[:, t, :], in_=z[:], func=ACT.Sigmoid, bias=bias[:, t : t + 1], scale=1.0)
+                conv_pass(q, t, z[:], slice(0, BANK))
+                sigmoid(q, t, slice(0, BANK), z[:])
 
-        def group_f(q):
-            f_grouped = stage.tile([P, BANK, PACK], BF16, align_bytes=64)
-            f_grouped_of[q] = f_grouped
-            regroup(nc.gpsimd, f_grouped[:], feat_of[q][:].rearrange("p t c -> p c t"))
+        def conv_half(q, half):
+            if half == 0:
+                feat = stage.tile([P, PACK, BANK], F32)
+                feat_of[q] = feat
+            columns = slice(half * HALF, (half + 1) * HALF)
+            for u in range(2):
+                z = scalar_psum.tile([P, PAIR, HALF], F32, tag="s")
+                for e in range(PAIR):
+                    conv_pass(q, PAIR * u + e, z[:, e, :], columns)
+                for e in range(PAIR):
+                    sigmoid(q, PAIR * u + e, columns, z[:, e, :])
 
-        def quantise_f(q):
-            f_codes = stage.tile([P, BANK], U32, align_bytes=64)
-            f_scales = stage.tile([P, BANK], U8, align_bytes=64)
-            f_codes_of[q] = f_codes
-            f_scales_of[q] = f_scales
+        def group_f(q, engine, columns=slice(0, BANK)):
+            if q not in f_grouped_of:
+                f_grouped = stage.tile([P, BANK, PACK], BF16, align_bytes=64)
+                f_grouped_of[q] = f_grouped
+            regroup(
+                engine, f_grouped_of[q][:, columns, :], feat_of[q][:, :, columns].rearrange("p t c -> p c t"), factor=-2.0
+            )
+
+        def quantise_f(q, columns=slice(0, BANK)):
+            if q not in f_codes_of:
+                f_codes = stage.tile([P, BANK], U32, align_bytes=64)
+                f_scales = stage.tile([P, BANK], U8, align_bytes=64)
+                f_codes_of[q] = f_codes
+                f_scales_of[q] = f_scales
             nc.vector.quantize_mx(
-                out=f_codes[:].bitcast(FP8X4),
-                scales=f_scales[:],
-                in_=f_grouped_of[q][:].rearrange("p c t -> p (c t)"),
+                out=f_codes_of[q][:, columns].bitcast(FP8X4),
+                scales=f_scales_of[q][:, columns],
+                in_=f_grouped_of[q][:, columns, :].rearrange("p c t -> p (c t)"),
             )
 
         def feature_norms(q, tiles):
@@ -193,9 +255,7 @@ def tile_protopnet_pa_kernel(tc, h_relu, conv2_w_words, conv2_w_scales, conv2_b,
             for j in tiles:
                 flipped = scalar_psum.tile([P, PACK, P], F32, tag="s")
                 for t in range(PACK):
-                    nc.tensor.transpose(
-                        out=flipped[:, t, :], in_=feat_of[q][:, t, j * P : (j + 1) * P], identity=ident_f32[:]
-                    )
+                    nc.tensor.transpose(out=flipped[:, t, :], in_=feat_of[q][:, t, j * P : (j + 1) * P], identity=ident[:])
                 squares = stage.tile([P, CHANNELS], BF16, tag="squares")
                 nc.scalar.activation(
                     out=squares[:],
@@ -204,14 +264,14 @@ def tile_protopnet_pa_kernel(tc, h_relu, conv2_w_words, conv2_w_scales, conv2_b,
                     accum_out=f2_of[q][:, j : j + 1],
                 )
 
-        def distances(q, j):
+        def distances(q, j, chunks=range(PROTO_CHUNKS)):
             g = q // CHUNKS_PER_GROUP
             first_of_group = q % CHUNKS_PER_GROUP == 0 and j == 0
-            if first_of_group:
+            if g not in running_min_of:
                 running_min = stage.tile([P, PROTOS], F32)
                 running_min_of[g] = running_min
             f2_column = f2_of[q][:, j : j + 1]
-            for c in range(PROTO_CHUNKS):
+            for c in chunks:
                 if first_of_group:
                     fp = scalar_psum.tile([P, BANK], F32, tag="s")
                 else:
@@ -240,7 +300,7 @@ def tile_protopnet_pa_kernel(tc, h_relu, conv2_w_words, conv2_w_scales, conv2_b,
                 for i in range(TILES_PER_CHUNK):
                     k = c * TILES_PER_CHUNK + i
                     nc.tensor.transpose(
-                        out=flipped[:, i, :], in_=running_min_of[g][:, k * P : (k + 1) * P], identity=ident_f32[:]
+                        out=flipped[:, i, :], in_=running_min_of[g][:, k * P : (k + 1) * P], identity=ident[:]
                     )
                 tiles = slice(c * TILES_PER_CHUNK, (c + 1) * TILES_PER_CHUNK)
                 nc.vector.tensor_reduce(
@@ -250,21 +310,57 @@ def tile_protopnet_pa_kernel(tc, h_relu, conv2_w_words, conv2_w_scales, conv2_b,
                     axis=AXIS.X,
                 )
 
-        group_h(0, nc.vector)
+        first, second = slice(0, HALF), slice(HALF, BANK)
+        group_first_h()
         quantise_h(0)
-        prepare_prototypes(0)
-        conv(0)
+        flip_prototypes(0, 0, False)
+        flip_prototypes(0, 1, False)
+        conv_half(0, 0)
+        conv_half(0, 1)
         group_h(1, nc.gpsimd)
-        prepare_prototypes(1)
-        prepare_prototypes(2)
-        group_f(0)
-        feature_norms(0, range(TILES_PER_CHUNK))
-        quantise_f(0)
-        prepare_prototypes(3)
+        quantise_prototypes(0)
+        flip_prototypes(1, 0, False)
+        group_f(0, nc.vector, first)
+        quantise_f(0, first)
+        flip_prototypes(1, 1, False)
+        group_f(0, nc.vector, second)
+        feature_norms(0, range(0, 2))
+        quantise_f(0, second)
+        quantise_prototypes(1)
+        distances(0, 0, (0,))
+        distances(0, 1, (0,))
+        feature_norms(0, range(2, 4))
         quantise_h(1)
+        distances(0, 0, (1,))
+        distances(0, 1, (1,))
+        flip_prototypes(2, 0, True)
+        flip_prototypes(2, 1, True)
+        distances(0, 2, (0,))
+        distances(0, 3, (0,))
+        conv(1)
+        group_f(1, nc.gpsimd)
+        quantise_prototypes(2)
+        distances(0, 2, (1,))
+        distances(0, 3, (1,))
+        flip_prototypes(3, 0, True)
+        flip_prototypes(3, 1, True)
+        distances(0, 0, (2,))
+        distances(0, 1, (2,))
+        quantise_prototypes(3)
+        distances(0, 2, (2,))
+        distances(0, 3, (2,))
+        feature_norms(1, range(0, 2))
+        distances(0, 0, (3,))
+        distances(0, 1, (3,))
+        feature_norms(1, range(2, 4))
+        distances(0, 2, (3,))
+        distances(0, 3, (3,))
+        quantise_f(1)
+        group_h(2, nc.gpsimd)
+        quantise_h(2)
 
-        for q in range(CHUNKS):
-            if q > 0 and q % CHUNKS_PER_GROUP == 0:
+        for q in range(1, CHUNKS):
+            if q % CHUNKS_PER_GROUP == 0:
                 fold_group(q // CHUNKS_PER_GROUP - 1)
             distances(q, 0)
             if q + 2 < CHUNKS:
@@ -272,7 +368,7 @@ def tile_protopnet_pa_kernel(tc, h_relu, conv2_w_words, conv2_w_scales, conv2_b,
             distances(q, 1)
             if q + 1 < CHUNKS:
                 conv(q + 1)
-                group_f(q + 1)
+                group_f(q + 1, nc.gpsimd)
             distances(q, 2)
             if q + 1 < CHUNKS:
                 feature_norms(q + 1, range(0, 2))
@@ -282,20 +378,21 @@ def tile_protopnet_pa_kernel(tc, h_relu, conv2_w_words, conv2_w_scales, conv2_b,
                 quantise_f(q + 1)
             if q + 2 < CHUNKS:
                 quantise_h(q + 2)
-            for k in range(q * NORMS_PER_CHUNK, (q + 1) * NORMS_PER_CHUNK):
+            for k in range((q - 1) * PROTO_TILES // (CHUNKS - 1), q * PROTO_TILES // (CHUNKS - 1)):
                 prototype_norm(k)
         fold_group(GROUPS - 1)
 
         nc.vector.tensor_tensor(
             out=result[:], in0=best[:], in1=p2[:].unsqueeze(1).to_broadcast([P, IMAGES, PROTO_TILES]), op=ALU.add
         )
+        result_rows = keep.tile([P, 2, P], F32)
         half = IMAGES // 2
         rows = vector_psum.tile([P, 2, P], F32, tag="v")
         for s in range(2):
             nc.tensor.transpose(
                 out=rows[:, s, :],
                 in_=result[:, s * half : (s + 1) * half, :].rearrange("p b k -> p (b k)"),
-                identity=ident_f32[:],
+                identity=ident[:],
             )
         nc.vector.tensor_copy(out=result_rows[:], in_=rows[:])
         for s in range(2):

@@ -339,6 +339,7 @@ def tile_protopnet_pa_kernel(tc, h_relu, conv2_w_words, conv2_w_scales, conv2_b,
         distances(0, 3, (0,))
         conv(1)
         group_f(1, nc.gpsimd)
+        group_h(2, nc.gpsimd)
         quantise_prototypes(2)
         distances(0, 2, (1,))
         distances(0, 3, (1,))
@@ -349,35 +350,37 @@ def tile_protopnet_pa_kernel(tc, h_relu, conv2_w_words, conv2_w_scales, conv2_b,
         quantise_prototypes(3)
         distances(0, 2, (2,))
         distances(0, 3, (2,))
-        feature_norms(1, range(0, 2))
+        feature_norms(1, (3, 2))
         distances(0, 0, (3,))
         distances(0, 1, (3,))
-        feature_norms(1, range(2, 4))
+        feature_norms(1, (1, 0))
+        quantise_f(1)
+        quantise_h(2)
         distances(0, 2, (3,))
         distances(0, 3, (3,))
-        quantise_f(1)
-        group_h(2, nc.gpsimd)
-        quantise_h(2)
 
         for q in range(1, CHUNKS):
             if q % CHUNKS_PER_GROUP == 0:
                 fold_group(q // CHUNKS_PER_GROUP - 1)
-            distances(q, 0)
+            else:
+                distances(q, 0)
             if q + 2 < CHUNKS:
                 group_h(q + 2, nc.gpsimd)
-            distances(q, 1)
             if q + 1 < CHUNKS:
                 conv(q + 1)
                 group_f(q + 1, nc.gpsimd)
+            distances(q, 1)
+            if q + 1 < CHUNKS:
+                feature_norms(q + 1, (3, 2))
             distances(q, 2)
             if q + 1 < CHUNKS:
-                feature_norms(q + 1, range(0, 2))
-            distances(q, 3)
-            if q + 1 < CHUNKS:
-                feature_norms(q + 1, range(2, 4))
+                feature_norms(q + 1, (1, 0))
                 quantise_f(q + 1)
             if q + 2 < CHUNKS:
                 quantise_h(q + 2)
+            distances(q, 3)
+            if q + 1 < CHUNKS and (q + 1) % CHUNKS_PER_GROUP == 0:
+                distances(q + 1, 0, range(PROTO_CHUNKS - 1, -1, -1))
             for k in range((q - 1) * PROTO_TILES // (CHUNKS - 1), q * PROTO_TILES // (CHUNKS - 1)):
                 prototype_norm(k)
         fold_group(GROUPS - 1)

@@ -33,7 +33,6 @@ CHUNKS_PER_GROUP = CHUNKS // GROUPS
 PROTO_TILES = PROTOS // P
 PROTO_CHUNKS = PROTOS // BANK
 FLIPS = BANK // (PAIR * P)
-WARMUPS = 8
 
 FLOPS = 2 * IMAGES * POSITIONS * CHANNELS * (CHANNELS + PROTOS)
 
@@ -86,37 +85,42 @@ def tile_protopnet_pa_kernel(tc, h_relu, conv2_w_words, conv2_w_scales, conv2_b,
                 out=w_scales_raw[32 * quadrant : 32 * quadrant + 4, :].bitcast(I32),
                 in_=scale_rows[4 * quadrant : 4 * quadrant + 4, :].bitcast(I32),
             )
-        nc.sync.dma_start(
-            out=w_codes_raw[:].bitcast(I32), in_=conv2_w_words.rearrange("g p n t -> (g p) (n t)").bitcast(I32)
-        )
         nc.scalar.dma_start(
             out=bias_rows[0 : CHANNELS // (PAIR * P), :].bitcast(BF16),
             in_=conv2_b.rearrange("(u i) -> u i", i=PAIR * P),
         )
         for b in range(GROUP_IMAGES):
             nc.sync.dma_start(out=h_raw[:, b], in_=h_view[:, b])
+        nc.sync.dma_start(
+            out=w_codes_raw[:].bitcast(I32), in_=conv2_w_words.rearrange("g p n t -> (g p) (n t)").bitcast(I32)
+        )
         for c in range(PROTO_CHUNKS):
             tiles = slice(c * TILES_PER_CHUNK, (c + 1) * TILES_PER_CHUNK)
             nc.sync.dma_start(out=p_raw[:, tiles, :], in_=p_view[:, tiles, :])
         for g in range(1, GROUPS):
             load_group(g)
 
-        nc.vector.tensor_copy(
-            out=w_codes[:].bitcast(I32).rearrange("p (u e m) -> p u e m", u=2, e=PAIR),
-            in_=w_codes_raw[:].bitcast(I32).rearrange("p (u m e) -> p u e m", u=2, e=PAIR),
-        )
-        nc.vector.tensor_copy(
-            out=w_scales[:].rearrange("p (u e m) -> p u e m", u=2, e=PAIR),
-            in_=w_scales_raw[:].rearrange("p (u m e) -> p u e m", u=2, e=PAIR),
-        )
+        def warm_up(products):
+            unread = scalar_psum.tile([P, BANK], F32, tag="s")
+            for i in range(products):
+                nc.tensor.matmul(out=unread[:], lhsT=zeros[:, 0:P], rhs=zeros[:], start=True, stop=True)
 
-        unread = scalar_psum.tile([P, BANK], F32, tag="s")
-        for i in range(WARMUPS):
-            nc.tensor.matmul(out=unread[:], lhsT=zeros[:, 0:P], rhs=zeros[:], start=True, stop=True)
+        def flip_bias():
+            flipped = vector_psum.tile([P, P], F32, tag="v")
+            nc.tensor.transpose(out=flipped[:], in_=bias_rows[:], identity=ident[:])
+            nc.vector.tensor_copy(out=bias[:], in_=flipped[:, 0 : PACK // PAIR].bitcast(BF16))
 
-        bias_flipped = vector_psum.tile([P, P], F32, tag="v")
-        nc.tensor.transpose(out=bias_flipped[:], in_=bias_rows[:], identity=ident[:])
-        nc.vector.tensor_copy(out=bias[:], in_=bias_flipped[:, 0 : PACK // PAIR].bitcast(BF16))
+        def order_w_codes():
+            nc.vector.tensor_copy(
+                out=w_codes[:].bitcast(I32).rearrange("p (u e m) -> p u e m", u=2, e=PAIR),
+                in_=w_codes_raw[:].bitcast(I32).rearrange("p (u m e) -> p u e m", u=2, e=PAIR),
+            )
+
+        def order_w_scales():
+            nc.vector.tensor_copy(
+                out=w_scales[:].rearrange("p (u e m) -> p u e m", u=2, e=PAIR),
+                in_=w_scales_raw[:].rearrange("p (u m e) -> p u e m", u=2, e=PAIR),
+            )
 
         h_grouped_of = {}
         p_grouped_of = {}
@@ -311,52 +315,59 @@ def tile_protopnet_pa_kernel(tc, h_relu, conv2_w_words, conv2_w_scales, conv2_b,
                 )
 
         first, second = slice(0, HALF), slice(HALF, BANK)
+        order_w_scales()
         group_first_h()
+        warm_up(6)
+        flip_bias()
+        warm_up(12)
         quantise_h(0)
-        flip_prototypes(0, 0, False)
-        flip_prototypes(0, 1, False)
+        order_w_codes()
         conv_half(0, 0)
+        flip_prototypes(0, 0, False)
         conv_half(0, 1)
-        group_h(1, nc.gpsimd)
-        quantise_prototypes(0)
+        flip_prototypes(0, 1, False)
+        group_f(0, nc.gpsimd, first)
+        group_f(0, nc.gpsimd, second)
+        warm_up(2)
         flip_prototypes(1, 0, False)
-        group_f(0, nc.vector, first)
-        quantise_f(0, first)
         flip_prototypes(1, 1, False)
-        group_f(0, nc.vector, second)
-        feature_norms(0, range(0, 2))
+        quantise_prototypes(0)
+        feature_norms(0, (1, 0))
+        quantise_f(0, first)
+        warm_up(2)
+        flip_prototypes(2, 0, False)
+        flip_prototypes(2, 1, False)
         quantise_f(0, second)
+        group_h(1, nc.gpsimd)
         quantise_prototypes(1)
         distances(0, 0, (0,))
-        distances(0, 1, (0,))
-        feature_norms(0, range(2, 4))
-        quantise_h(1)
-        distances(0, 0, (1,))
-        distances(0, 1, (1,))
-        flip_prototypes(2, 0, True)
-        flip_prototypes(2, 1, True)
-        distances(0, 2, (0,))
-        distances(0, 3, (0,))
-        conv(1)
-        group_f(1, nc.gpsimd)
-        group_h(2, nc.gpsimd)
-        quantise_prototypes(2)
-        distances(0, 2, (1,))
-        distances(0, 3, (1,))
+        feature_norms(0, (3, 2))
         flip_prototypes(3, 0, True)
         flip_prototypes(3, 1, True)
-        distances(0, 0, (2,))
-        distances(0, 1, (2,))
+        quantise_prototypes(2)
+        distances(0, 1, (0,))
+        distances(0, 2, (0,))
+        distances(0, 3, (0,))
+        quantise_h(1)
+        distances(0, 0, (1,))
         quantise_prototypes(3)
+        distances(0, 1, (1,))
+        distances(0, 2, (1,))
+        distances(0, 3, (1,))
+        conv(1)
+        group_h(2, nc.gpsimd)
+        group_f(1, nc.gpsimd)
+        distances(0, 0, (2,))
+        distances(0, 0, (3,))
+        distances(0, 1, (2,))
         distances(0, 2, (2,))
         distances(0, 3, (2,))
         feature_norms(1, (3, 2))
-        distances(0, 0, (3,))
         distances(0, 1, (3,))
         feature_norms(1, (1, 0))
+        distances(0, 2, (3,))
         quantise_f(1)
         quantise_h(2)
-        distances(0, 2, (3,))
         distances(0, 3, (3,))
 
         for q in range(1, CHUNKS):

@@ -20,6 +20,7 @@ BANK = 512
 HALF = BANK // 2
 
 IMAGES = 16
+HALF_IMAGES = IMAGES // 2
 CHANNELS = 512
 POSITIONS = 256
 PROTOS = 2048
@@ -61,7 +62,6 @@ def tile_protopnet_pa_kernel(tc, h_relu, conv2_w_words, conv2_w_scales, conv2_b,
         bias = keep.tile([P, PACK], F32)
         p2 = keep.tile([P, PROTO_TILES], F32)
         best = keep.tile([P, IMAGES, PROTO_TILES], F32)
-        result = keep.tile([P, IMAGES, PROTO_TILES], F32)
         table_warmer = keep.tile([P, 1], F32)
         zeros = keep.tile([P, BANK], BF16)
 
@@ -130,6 +130,7 @@ def tile_protopnet_pa_kernel(tc, h_relu, conv2_w_words, conv2_w_scales, conv2_b,
         f_scales_of = {}
         f2_of = {}
         running_min_of = {}
+        f2_gap_of = {}
 
         def regroup(engine, dst, src, factor=1.0):
             engine.tensor_scalar(out=dst, in0=src, scalar1=factor, scalar2=0.0, op0=ALU.mult, op1=ALU.add)
@@ -144,7 +145,7 @@ def tile_protopnet_pa_kernel(tc, h_relu, conv2_w_words, conv2_w_scales, conv2_b,
             for b in range(GROUP_IMAGES):
                 regroup(nc.vector, by_image[:, b], h_raw[:, b, :, 0:P].rearrange("p t (j r) -> p j r t", r=RUN))
 
-        def group_h(q, engine):
+        def group_h(q):
             new_h_grouped(q)
             g = q // CHUNKS_PER_GROUP
             images = slice(g * GROUP_IMAGES, (g + 1) * GROUP_IMAGES)
@@ -152,7 +153,7 @@ def tile_protopnet_pa_kernel(tc, h_relu, conv2_w_words, conv2_w_scales, conv2_b,
                 tile_in_group = (q % CHUNKS_PER_GROUP) * TILES_PER_CHUNK + j
                 run = slice(tile_in_group * RUN, (tile_in_group + 1) * RUN)
                 regroup(
-                    engine,
+                    nc.gpsimd,
                     h_grouped_of[q][:, j * P : (j + 1) * P, :].rearrange("p (b r) t -> p b r t", r=RUN),
                     h_raw[:, images, :, run].rearrange("p b t r -> p b r t"),
                 )
@@ -232,18 +233,25 @@ def tile_protopnet_pa_kernel(tc, h_relu, conv2_w_words, conv2_w_scales, conv2_b,
                 for e in range(PAIR):
                     sigmoid(q, PAIR * u + e, columns, z[:, e, :])
 
-        def group_f(q, engine, columns=slice(0, BANK)):
+        def group_f(q, columns=slice(0, BANK), factor=-2.0):
             if q not in f_grouped_of:
                 f_grouped = stage.tile([P, BANK, PACK], BF16, align_bytes=64)
                 f_grouped_of[q] = f_grouped
             regroup(
-                engine, f_grouped_of[q][:, columns, :], feat_of[q][:, :, columns].rearrange("p t c -> p c t"), factor=-2.0
+                nc.gpsimd,
+                f_grouped_of[q][:, columns, :],
+                feat_of[q][:, :, columns].rearrange("p t c -> p c t"),
+                factor=factor,
             )
+
+        def group_paired_f(q):
+            group_f(q, slice(0, P), 2.0)
+            group_f(q, slice(P, BANK))
 
         def quantise_f(q, columns=slice(0, BANK)):
             if q not in f_codes_of:
-                f_codes = stage.tile([P, BANK], U32, align_bytes=64)
-                f_scales = stage.tile([P, BANK], U8, align_bytes=64)
+                f_codes = stage.tile([P, BANK], U32, align_bytes=64, bufs=3)
+                f_scales = stage.tile([P, BANK], U8, align_bytes=64, bufs=3)
                 f_codes_of[q] = f_codes
                 f_scales_of[q] = f_scales
             nc.vector.quantize_mx(
@@ -254,7 +262,7 @@ def tile_protopnet_pa_kernel(tc, h_relu, conv2_w_words, conv2_w_scales, conv2_b,
 
         def feature_norms(q, tiles):
             if q not in f2_of:
-                f2 = stage.tile([P, TILES_PER_CHUNK], F32)
+                f2 = stage.tile([P, TILES_PER_CHUNK], F32, bufs=3)
                 f2_of[q] = f2
             for j in tiles:
                 flipped = scalar_psum.tile([P, PACK, P], F32, tag="s")
@@ -268,6 +276,37 @@ def tile_protopnet_pa_kernel(tc, h_relu, conv2_w_words, conv2_w_scales, conv2_b,
                     accum_out=f2_of[q][:, j : j + 1],
                 )
 
+        def product(q, j, c, fp, start=True, stop=True):
+            nc.tensor.matmul_mx(
+                out=fp[:],
+                lhsT=f_codes_of[q][:, j * P : (j + 1) * P].bitcast(FP8X4),
+                lhsT_scale=f_scales_of[q][:, j * P : (j + 1) * P],
+                rhs=p_codes[:, c, :].bitcast(FP8X4),
+                rhs_scale=p_scales[:, c, :],
+                start=start,
+                stop=stop,
+            )
+
+        def begin_pair(q):
+            f2_gap = stage.tile([P, 1], F32)
+            f2_gap_of[q] = f2_gap
+            f2 = f2_of[q]
+            nc.scalar.activation(out=f2_gap[:], in_=f2[:, 0:1], func=ACT.Identity, bias=f2[:, 1:2], scale=-1.0)
+
+        def pair_minimum(q, c, kept):
+            fp = scalar_psum.tile([P, BANK], F32, tag="s")
+            product(q, 1, c, fp)
+            nc.scalar.activation(out=kept, in_=fp[:], func=ACT.Identity, bias=f2_of[q][:, 1:2], scale=1.0)
+            gap = scalar_psum.tile([P, BANK], F32, tag="s")
+            product(q, 1, c, gap, stop=False)
+            product(q, 0, c, gap, start=False)
+            excess = stage.tile([P, BANK], F32, bufs=4)
+            nc.scalar.activation(out=excess[:], in_=gap[:], func=ACT.Relu, bias=f2_gap_of[q][:], scale=1.0)
+            nc.gpsimd.tensor_tensor(out=kept, in0=kept, in1=excess[:], op=ALU.subtract)
+
+        def bank(tile, c):
+            return tile[:, c * BANK : (c + 1) * BANK]
+
         def distances(q, j, chunks=range(PROTO_CHUNKS)):
             g = q // CHUNKS_PER_GROUP
             first_of_group = q % CHUNKS_PER_GROUP == 0 and j == 0
@@ -280,15 +319,7 @@ def tile_protopnet_pa_kernel(tc, h_relu, conv2_w_words, conv2_w_scales, conv2_b,
                     fp = scalar_psum.tile([P, BANK], F32, tag="s")
                 else:
                     fp = vector_psum.tile([P, BANK], F32, tag="v")
-                nc.tensor.matmul_mx(
-                    out=fp[:],
-                    lhsT=f_codes_of[q][:, j * P : (j + 1) * P].bitcast(FP8X4),
-                    lhsT_scale=f_scales_of[q][:, j * P : (j + 1) * P],
-                    rhs=p_codes[:, c, :].bitcast(FP8X4),
-                    rhs_scale=p_scales[:, c, :],
-                    start=True,
-                    stop=True,
-                )
+                product(q, j, c, fp)
                 kept = running_min_of[g][:, c * BANK : (c + 1) * BANK]
                 if first_of_group:
                     nc.scalar.activation(out=kept, in_=fp[:], func=ACT.Identity, bias=f2_column, scale=1.0)
@@ -297,9 +328,9 @@ def tile_protopnet_pa_kernel(tc, h_relu, conv2_w_words, conv2_w_scales, conv2_b,
                         out=kept, in0=fp[:], scalar=f2_column, in1=kept, op0=ALU.add, op1=ALU.min
                     )
 
-        def fold_group(g):
+        def fold_group(g, chunks=range(PROTO_CHUNKS)):
             images = slice(g * GROUP_IMAGES, (g + 1) * GROUP_IMAGES)
-            for c in range(PROTO_CHUNKS):
+            for c in chunks:
                 flipped = vector_psum.tile([P, TILES_PER_CHUNK, P], F32, tag="v")
                 for i in range(TILES_PER_CHUNK):
                     k = c * TILES_PER_CHUNK + i
@@ -314,20 +345,44 @@ def tile_protopnet_pa_kernel(tc, h_relu, conv2_w_words, conv2_w_scales, conv2_b,
                     axis=AXIS.X,
                 )
 
+        result_of = {}
+        rows_of = {}
+
+        def add_p2(s):
+            result = stage.tile([P, HALF_IMAGES, PROTO_TILES], F32)
+            result_of[s] = result
+            nc.vector.tensor_tensor(
+                out=result[:],
+                in0=best[:, s * HALF_IMAGES : (s + 1) * HALF_IMAGES, :],
+                in1=p2[:].unsqueeze(1).to_broadcast([P, HALF_IMAGES, PROTO_TILES]),
+                op=ALU.add,
+            )
+
+        def flip_result(s):
+            rows = vector_psum.tile([P, P], F32, tag="v")
+            rows_of[s] = rows
+            nc.tensor.transpose(out=rows[:], in_=result_of[s][:].rearrange("p b k -> p (b k)"), identity=ident[:])
+
+        def store_result(s):
+            result_rows = stage.tile([P, P], F32)
+            nc.vector.tensor_copy(out=result_rows[:], in_=rows_of[s][:])
+            images = slice(s * HALF_IMAGES, (s + 1) * HALF_IMAGES)
+            nc.sync.dma_start(out=out[images, :].rearrange("b (k r) -> (b k) r", r=P), in_=result_rows[:])
+
         first, second = slice(0, HALF), slice(HALF, BANK)
         order_w_scales()
         group_first_h()
         warm_up(6)
         flip_bias()
-        warm_up(12)
+        warm_up(6)
         quantise_h(0)
         order_w_codes()
         conv_half(0, 0)
         flip_prototypes(0, 0, False)
         conv_half(0, 1)
         flip_prototypes(0, 1, False)
-        group_f(0, nc.gpsimd, first)
-        group_f(0, nc.gpsimd, second)
+        group_f(0, first)
+        group_f(0, second)
         warm_up(2)
         flip_prototypes(1, 0, False)
         flip_prototypes(1, 1, False)
@@ -338,28 +393,28 @@ def tile_protopnet_pa_kernel(tc, h_relu, conv2_w_words, conv2_w_scales, conv2_b,
         flip_prototypes(2, 0, False)
         flip_prototypes(2, 1, False)
         quantise_f(0, second)
-        group_h(1, nc.gpsimd)
+        group_h(1)
         quantise_prototypes(1)
         distances(0, 0, (0,))
-        feature_norms(0, (3, 2))
-        flip_prototypes(3, 0, True)
-        flip_prototypes(3, 1, True)
-        quantise_prototypes(2)
         distances(0, 1, (0,))
+        feature_norms(0, (3, 2))
+        quantise_prototypes(2)
+        distances(0, 0, (1,))
+        flip_prototypes(3, 0, True)
         distances(0, 2, (0,))
         distances(0, 3, (0,))
+        flip_prototypes(3, 1, True)
         quantise_h(1)
-        distances(0, 0, (1,))
-        quantise_prototypes(3)
+        distances(0, 0, (2,))
         distances(0, 1, (1,))
         distances(0, 2, (1,))
+        quantise_prototypes(3)
         distances(0, 3, (1,))
         conv(1)
-        group_h(2, nc.gpsimd)
-        group_f(1, nc.gpsimd)
-        distances(0, 0, (2,))
-        distances(0, 0, (3,))
+        group_h(2)
+        group_f(1)
         distances(0, 1, (2,))
+        distances(0, 0, (3,))
         distances(0, 2, (2,))
         distances(0, 3, (2,))
         feature_norms(1, (3, 2))
@@ -370,46 +425,46 @@ def tile_protopnet_pa_kernel(tc, h_relu, conv2_w_words, conv2_w_scales, conv2_b,
         quantise_h(2)
         distances(0, 3, (3,))
 
-        for q in range(1, CHUNKS):
+        last = CHUNKS - 1
+        for q in range(1, last):
             if q % CHUNKS_PER_GROUP == 0:
                 fold_group(q // CHUNKS_PER_GROUP - 1)
             else:
                 distances(q, 0)
-            if q + 2 < CHUNKS:
-                group_h(q + 2, nc.gpsimd)
-            if q + 1 < CHUNKS:
-                conv(q + 1)
-                group_f(q + 1, nc.gpsimd)
+            if q + 1 < last:
+                group_h(q + 2)
+            conv(q + 1)
+            if q + 1 < last:
+                group_f(q + 1)
+            else:
+                group_paired_f(last)
             distances(q, 1)
-            if q + 1 < CHUNKS:
-                feature_norms(q + 1, (3, 2))
+            feature_norms(q + 1, (3, 2))
             distances(q, 2)
-            if q + 1 < CHUNKS:
-                feature_norms(q + 1, (1, 0))
-                quantise_f(q + 1)
-            if q + 2 < CHUNKS:
+            feature_norms(q + 1, (1, 0))
+            quantise_f(q + 1)
+            if q + 1 < last:
                 quantise_h(q + 2)
             distances(q, 3)
-            if q + 1 < CHUNKS and (q + 1) % CHUNKS_PER_GROUP == 0:
+            if (q + 1) % CHUNKS_PER_GROUP == 0:
                 distances(q + 1, 0, range(PROTO_CHUNKS - 1, -1, -1))
-            for k in range((q - 1) * PROTO_TILES // (CHUNKS - 1), q * PROTO_TILES // (CHUNKS - 1)):
-                prototype_norm(k)
-        fold_group(GROUPS - 1)
+            if q + 1 < last:
+                for k in range((q - 1) * 2, q * 2):
+                    prototype_norm(k)
 
-        nc.vector.tensor_tensor(
-            out=result[:], in0=best[:], in1=p2[:].unsqueeze(1).to_broadcast([P, IMAGES, PROTO_TILES]), op=ALU.add
-        )
-        result_rows = keep.tile([P, 2, P], F32)
-        half = IMAGES // 2
-        rows = vector_psum.tile([P, 2, P], F32, tag="v")
+        begin_pair(last)
+        paired = keep.tile([P, PROTOS], F32)
+        kept = running_min_of[GROUPS - 1]
+        for c in range(PROTO_CHUNKS):
+            pair_minimum(last, c, bank(paired, c))
+            distances(last, 2, (c,))
+        distances(last, 3)
+        for k in range(2 * (last - 2), PROTO_TILES):
+            prototype_norm(k)
+        for c in range(PROTO_CHUNKS):
+            nc.vector.tensor_tensor(out=bank(kept, c), in0=bank(kept, c), in1=bank(paired, c), op=ALU.min)
+        fold_group(GROUPS - 1)
         for s in range(2):
-            nc.tensor.transpose(
-                out=rows[:, s, :],
-                in_=result[:, s * half : (s + 1) * half, :].rearrange("p b k -> p (b k)"),
-                identity=ident[:],
-            )
-        nc.vector.tensor_copy(out=result_rows[:], in_=rows[:])
-        for s in range(2):
-            nc.sync.dma_start(
-                out=out[s * half : (s + 1) * half, :].rearrange("b (k r) -> (b k) r", r=P), in_=result_rows[:, s, :]
-            )
+            add_p2(s)
+            flip_result(s)
+            store_result(s)

@@ -79,17 +79,19 @@ def tile_protopnet_pa_kernel(tc, h_relu, conv2_w_words, conv2_w_scales, conv2_b,
             images = slice(g * GROUP_IMAGES, (g + 1) * GROUP_IMAGES)
             nc.sync.dma_start(out=h_raw[:, images], in_=h_view[:, images])
 
+        nc.scalar.dma_start(
+            out=bias_rows[0 : CHANNELS // (PAIR * P), :].bitcast(BF16),
+            in_=conv2_b.rearrange("(u i) -> u i", i=PAIR * P),
+        )
+        for b in range(0, 2):
+            nc.sync.dma_start(out=h_raw[:, b], in_=h_view[:, b])
         scale_rows = conv2_w_scales.rearrange("g q n -> (g q) n")
         for quadrant in range(4):
             nc.sync.dma_start(
                 out=w_scales_raw[32 * quadrant : 32 * quadrant + 4, :].bitcast(I32),
                 in_=scale_rows[4 * quadrant : 4 * quadrant + 4, :].bitcast(I32),
             )
-        nc.scalar.dma_start(
-            out=bias_rows[0 : CHANNELS // (PAIR * P), :].bitcast(BF16),
-            in_=conv2_b.rearrange("(u i) -> u i", i=PAIR * P),
-        )
-        for b in range(GROUP_IMAGES):
+        for b in range(2, GROUP_IMAGES):
             nc.sync.dma_start(out=h_raw[:, b], in_=h_view[:, b])
         nc.sync.dma_start(
             out=w_codes_raw[:].bitcast(I32), in_=conv2_w_words.rearrange("g p n t -> (g p) (n t)").bitcast(I32)
@@ -139,13 +141,14 @@ def tile_protopnet_pa_kernel(tc, h_relu, conv2_w_words, conv2_w_scales, conv2_b,
             h_grouped = stage.tile([P, BANK, PACK], BF16, align_bytes=64, bufs=1)
             h_grouped_of[q] = h_grouped
 
-        def group_first_h():
-            new_h_grouped(0)
+        def group_first_h(images):
+            if 0 not in h_grouped_of:
+                new_h_grouped(0)
             by_image = h_grouped_of[0][:].rearrange("p (j b r) t -> p b j r t", b=GROUP_IMAGES, r=RUN)
-            for b in range(GROUP_IMAGES):
+            for b in images:
                 regroup(nc.vector, by_image[:, b], h_raw[:, b, :, 0:P].rearrange("p t (j r) -> p j r t", r=RUN))
 
-        def group_h(q):
+        def group_h(q, engine=nc.gpsimd):
             new_h_grouped(q)
             g = q // CHUNKS_PER_GROUP
             images = slice(g * GROUP_IMAGES, (g + 1) * GROUP_IMAGES)
@@ -153,7 +156,7 @@ def tile_protopnet_pa_kernel(tc, h_relu, conv2_w_words, conv2_w_scales, conv2_b,
                 tile_in_group = (q % CHUNKS_PER_GROUP) * TILES_PER_CHUNK + j
                 run = slice(tile_in_group * RUN, (tile_in_group + 1) * RUN)
                 regroup(
-                    nc.gpsimd,
+                    engine,
                     h_grouped_of[q][:, j * P : (j + 1) * P, :].rearrange("p (b r) t -> p b r t", r=RUN),
                     h_raw[:, images, :, run].rearrange("p b t r -> p b r t"),
                 )
@@ -233,12 +236,12 @@ def tile_protopnet_pa_kernel(tc, h_relu, conv2_w_words, conv2_w_scales, conv2_b,
                 for e in range(PAIR):
                     sigmoid(q, PAIR * u + e, columns, z[:, e, :])
 
-        def group_f(q, columns=slice(0, BANK), factor=-2.0):
+        def group_f(q, columns=slice(0, BANK), factor=-2.0, engine=nc.gpsimd):
             if q not in f_grouped_of:
                 f_grouped = stage.tile([P, BANK, PACK], BF16, align_bytes=64)
                 f_grouped_of[q] = f_grouped
             regroup(
-                nc.gpsimd,
+                engine,
                 f_grouped_of[q][:, columns, :],
                 feat_of[q][:, :, columns].rearrange("p t c -> p c t"),
                 factor=factor,
@@ -303,6 +306,16 @@ def tile_protopnet_pa_kernel(tc, h_relu, conv2_w_words, conv2_w_scales, conv2_b,
             excess = stage.tile([P, BANK], F32, bufs=4)
             nc.scalar.activation(out=excess[:], in_=gap[:], func=ACT.Relu, bias=f2_gap_of[q][:], scale=1.0)
             nc.gpsimd.tensor_tensor(out=kept, in0=kept, in1=excess[:], op=ALU.subtract)
+
+        def split_minimum(q, c, kept):
+            fp = scalar_psum.tile([P, BANK], F32, tag="s")
+            product(q, 0, c, fp)
+            nc.scalar.activation(out=kept, in_=fp[:], func=ACT.Identity, bias=f2_of[q][:, 0:1], scale=-1.0)
+            other = vector_psum.tile([P, BANK], F32, tag="v")
+            product(q, 1, c, other)
+            nc.vector.scalar_tensor_tensor(
+                out=kept, in0=other[:], scalar=f2_of[q][:, 1:2], in1=kept, op0=ALU.add, op1=ALU.min
+            )
 
         def bank(tile, c):
             return tile[:, c * BANK : (c + 1) * BANK]
@@ -370,62 +383,64 @@ def tile_protopnet_pa_kernel(tc, h_relu, conv2_w_words, conv2_w_scales, conv2_b,
             nc.sync.dma_start(out=out[images, :].rearrange("b (k r) -> (b k) r", r=P), in_=result_rows[:])
 
         first, second = slice(0, HALF), slice(HALF, BANK)
+        group_first_h((0, 1))
         order_w_scales()
-        group_first_h()
+        group_first_h((2, 3))
         warm_up(6)
         flip_bias()
         warm_up(6)
         quantise_h(0)
         order_w_codes()
+        group_h(1, nc.vector)
         conv_half(0, 0)
         flip_prototypes(0, 0, False)
         conv_half(0, 1)
         flip_prototypes(0, 1, False)
-        group_f(0, first)
-        group_f(0, second)
+        group_f(0, first, engine=nc.vector)
         warm_up(2)
+        quantise_f(0, first)
         flip_prototypes(1, 0, False)
-        flip_prototypes(1, 1, False)
         quantise_prototypes(0)
         feature_norms(0, (1, 0))
-        quantise_f(0, first)
+        group_f(0, second, engine=nc.vector)
+        flip_prototypes(1, 1, False)
+        distances(0, 0, (0,))
+        quantise_f(0, second)
+        quantise_h(1)
         warm_up(2)
         flip_prototypes(2, 0, False)
         flip_prototypes(2, 1, False)
-        quantise_f(0, second)
-        group_h(1)
         quantise_prototypes(1)
-        distances(0, 0, (0,))
         distances(0, 1, (0,))
         feature_norms(0, (3, 2))
-        quantise_prototypes(2)
         distances(0, 0, (1,))
-        flip_prototypes(3, 0, True)
+        quantise_prototypes(2)
+        group_h(2)
         distances(0, 2, (0,))
         distances(0, 3, (0,))
+        flip_prototypes(3, 0, True)
         flip_prototypes(3, 1, True)
-        quantise_h(1)
-        distances(0, 0, (2,))
         distances(0, 1, (1,))
         distances(0, 2, (1,))
-        quantise_prototypes(3)
         distances(0, 3, (1,))
+        distances(0, 0, (2,))
         conv(1)
-        group_h(2)
         group_f(1)
+        quantise_prototypes(3)
         distances(0, 1, (2,))
-        distances(0, 0, (3,))
         distances(0, 2, (2,))
         distances(0, 3, (2,))
-        feature_norms(1, (3, 2))
+        distances(0, 0, (3,))
+        feature_norms(1, (0, 1))
         distances(0, 1, (3,))
-        feature_norms(1, (1, 0))
         distances(0, 2, (3,))
+        feature_norms(1, (2, 3))
         quantise_f(1)
         quantise_h(2)
         distances(0, 3, (3,))
 
         last = CHUNKS - 1
+        norms = 0
         for q in range(1, last):
             if q % CHUNKS_PER_GROUP == 0:
                 fold_group(q // CHUNKS_PER_GROUP - 1)
@@ -439,32 +454,37 @@ def tile_protopnet_pa_kernel(tc, h_relu, conv2_w_words, conv2_w_scales, conv2_b,
             else:
                 group_paired_f(last)
             distances(q, 1)
-            feature_norms(q + 1, (3, 2))
+            for k in range(norms, norms + (4 if q % CHUNKS_PER_GROUP else 2)):
+                if k < PROTO_TILES:
+                    prototype_norm(k)
+            norms += 4 if q % CHUNKS_PER_GROUP else 2
             distances(q, 2)
-            feature_norms(q + 1, (1, 0))
+            feature_norms(q + 1, (0, 1))
+            distances(q, 3, (0, 1))
             quantise_f(q + 1)
             if q + 1 < last:
                 quantise_h(q + 2)
-            distances(q, 3)
+            else:
+                add_p2(0)
+            feature_norms(q + 1, (2, 3))
+            distances(q, 3, (2, 3))
             if (q + 1) % CHUNKS_PER_GROUP == 0:
                 distances(q + 1, 0, range(PROTO_CHUNKS - 1, -1, -1))
-            if q + 1 < last:
-                for k in range((q - 1) * 2, q * 2):
-                    prototype_norm(k)
 
         begin_pair(last)
         paired = keep.tile([P, PROTOS], F32)
         kept = running_min_of[GROUPS - 1]
         for c in range(PROTO_CHUNKS):
-            pair_minimum(last, c, bank(paired, c))
+            if c + 1 < PROTO_CHUNKS:
+                pair_minimum(last, c, bank(paired, c))
             distances(last, 2, (c,))
-        distances(last, 3)
-        for k in range(2 * (last - 2), PROTO_TILES):
-            prototype_norm(k)
+            distances(last, 3, (c,))
+        split_minimum(last, PROTO_CHUNKS - 1, bank(paired, PROTO_CHUNKS - 1))
+        flip_result(0)
         for c in range(PROTO_CHUNKS):
             nc.vector.tensor_tensor(out=bank(kept, c), in0=bank(kept, c), in1=bank(paired, c), op=ALU.min)
         fold_group(GROUPS - 1)
-        for s in range(2):
-            add_p2(s)
-            flip_result(s)
-            store_result(s)
+        store_result(0)
+        add_p2(1)
+        flip_result(1)
+        store_result(1)

@@ -404,26 +404,25 @@ def tile_protopnet_pa_kernel(tc, h_relu, conv2_w_words, conv2_w_scales, conv2_b,
         feature_norms(0, (1, 0))
         group_f(0, second, engine=nc.vector)
         flip_prototypes(1, 1, False)
-        distances(0, 0, (0,))
+        flip_prototypes(2, 0, True)
+        flip_prototypes(2, 1, True)
         quantise_f(0, second)
-        quantise_h(1)
-        warm_up(2)
-        flip_prototypes(2, 0, False)
-        flip_prototypes(2, 1, False)
+        distances(0, 0, (0,))
         quantise_prototypes(1)
         distances(0, 1, (0,))
         feature_norms(0, (3, 2))
-        distances(0, 0, (1,))
+        flip_prototypes(3, 0, True)
+        flip_prototypes(3, 1, True)
+        quantise_h(1)
         quantise_prototypes(2)
         group_h(2)
         distances(0, 2, (0,))
         distances(0, 3, (0,))
-        flip_prototypes(3, 0, True)
-        flip_prototypes(3, 1, True)
+        distances(0, 0, (1,))
         distances(0, 1, (1,))
+        distances(0, 0, (2,))
         distances(0, 2, (1,))
         distances(0, 3, (1,))
-        distances(0, 0, (2,))
         conv(1)
         group_f(1)
         quantise_prototypes(3)

@@ -170,7 +170,7 @@ def tile_protopnet_pa_kernel(tc, h_relu, conv2_w_words, conv2_w_scales, conv2_b,
 
         def flip_prototypes(c, pair, on_scalar):
             if c not in p_grouped_of:
-                p_grouped = stage.tile([P, BANK, PACK], BF16, align_bytes=64)
+                p_grouped = stage.tile([P, BANK, PACK], BF16, align_bytes=64, bufs=PROTO_CHUNKS)
                 p_grouped_of[c] = p_grouped
             if on_scalar:
                 flipped = scalar_psum.tile([P, FLIPS, 2, P], F32, tag="s")
@@ -388,22 +388,23 @@ def tile_protopnet_pa_kernel(tc, h_relu, conv2_w_words, conv2_w_scales, conv2_b,
         group_first_h((2, 3))
         warm_up(6)
         flip_bias()
-        warm_up(6)
+        warm_up(10)
         quantise_h(0)
         order_w_codes()
         group_h(1, nc.vector)
         conv_half(0, 0)
         flip_prototypes(0, 0, False)
-        conv_half(0, 1)
         flip_prototypes(0, 1, False)
+        conv_half(0, 1)
         group_f(0, first, engine=nc.vector)
         warm_up(2)
         quantise_f(0, first)
-        flip_prototypes(1, 0, False)
         quantise_prototypes(0)
+        flip_prototypes(1, 0, False)
         feature_norms(0, (1, 0))
         group_f(0, second, engine=nc.vector)
         flip_prototypes(1, 1, False)
+        warm_up(2)
         flip_prototypes(2, 0, True)
         flip_prototypes(2, 1, True)
         quantise_f(0, second)
@@ -483,7 +484,7 @@ def tile_protopnet_pa_kernel(tc, h_relu, conv2_w_words, conv2_w_scales, conv2_b,
         for c in range(PROTO_CHUNKS):
             nc.vector.tensor_tensor(out=bank(kept, c), in0=bank(kept, c), in1=bank(paired, c), op=ALU.min)
         fold_group(GROUPS - 1)
-        store_result(0)
         add_p2(1)
         flip_result(1)
+        store_result(0)
         store_result(1)

@@ -460,14 +460,14 @@ def tile_protopnet_pa_kernel(tc, h_relu, conv2_w_words, conv2_w_scales, conv2_b,
             norms += 4 if q % CHUNKS_PER_GROUP else 2
             distances(q, 2)
             feature_norms(q + 1, (0, 1))
-            distances(q, 3, (0, 1))
+            distances(q, 3, (0,))
             quantise_f(q + 1)
             if q + 1 < last:
                 quantise_h(q + 2)
             else:
                 add_p2(0)
             feature_norms(q + 1, (2, 3))
-            distances(q, 3, (2, 3))
+            distances(q, 3, (1, 2, 3))
             if (q + 1) % CHUNKS_PER_GROUP == 0:
                 distances(q + 1, 0, range(PROTO_CHUNKS - 1, -1, -1))
 

from contextlib import ExitStack

import concourse.mybir as mybir
from concourse.masks import make_identity

BF16 = mybir.dt.bfloat16
F32 = mybir.dt.float32
I32 = mybir.dt.int32
U32 = mybir.dt.uint32
U8 = mybir.dt.uint8
FP8X4 = mybir.dt.float8_e4m3fn_x4
ALU = mybir.AluOpType
ACT = mybir.ActivationFunctionType
AXIS = mybir.AxisListType

P = 128
PACK = 4
PAIR = 2
BANK = 512
HALF = BANK // 2

IMAGES = 16
HALF_IMAGES = IMAGES // 2
CHANNELS = 512
POSITIONS = 256
PROTOS = 2048

GROUP_IMAGES = 4
RUN = P // GROUP_IMAGES
GROUPS = IMAGES // GROUP_IMAGES
TILES_PER_CHUNK = BANK // P
CHUNKS = IMAGES * POSITIONS // BANK
CHUNKS_PER_GROUP = CHUNKS // GROUPS
PROTO_TILES = PROTOS // P
PROTO_CHUNKS = PROTOS // BANK
FLIPS = BANK // (PAIR * P)

FLOPS = 2 * IMAGES * POSITIONS * CHANNELS * (CHANNELS + PROTOS)


def tile_protopnet_pa_kernel(tc, h_relu, conv2_w_words, conv2_w_scales, conv2_b, prototypes, out):
    nc = tc.nc
    with ExitStack() as ctx:
        keep = ctx.enter_context(tc.tile_pool(name="keep", bufs=1))
        stage = ctx.enter_context(tc.tile_pool(name="stage", bufs=2))
        scalar_psum = ctx.enter_context(tc.psum_pool(name="scalar_psum", bufs=4))
        vector_psum = ctx.enter_context(tc.psum_pool(name="vector_psum", bufs=4))
        ctx.enter_context(tc.manual_schedule())

        h_raw = keep.tile([P, IMAGES, PACK, POSITIONS], BF16)
        p_raw = keep.tile([P, PROTO_TILES, CHANNELS], BF16)
        w_codes_raw = keep.tile([P, CHANNELS], U32, align_bytes=64)
        w_scales_raw = keep.tile([P, CHANNELS], U8, align_bytes=64)
        w_codes = keep.tile([P, CHANNELS], U32, align_bytes=64)
        w_scales = keep.tile([P, CHANNELS], U8, align_bytes=64)
        h_codes = keep.tile([P, CHUNKS, BANK], U32, align_bytes=64)
        h_scales = keep.tile([P, CHUNKS, BANK], U8, align_bytes=64)
        p_codes = keep.tile([P, PROTO_CHUNKS, BANK], U32, align_bytes=64)
        p_scales = keep.tile([P, PROTO_CHUNKS, BANK], U8, align_bytes=64)
        ident = keep.tile([P, P], F32)
        bias_rows = keep.tile([P, P], F32)
        bias = keep.tile([P, PACK], F32)
        p2 = keep.tile([P, PROTO_TILES], F32)
        best = keep.tile([P, IMAGES, PROTO_TILES], F32)
        table_warmer = keep.tile([P, 1], F32)
        zeros = keep.tile([P, BANK], BF16)

        nc.vector.memset(w_scales_raw[:].bitcast(I32), 0)
        nc.vector.memset(zeros[:], 0.0)
        nc.vector.memset(bias_rows[:], 0.0)
        nc.vector.memset(table_warmer[:], 0.0)
        nc.scalar.activation(out=table_warmer[:], in_=table_warmer[:], func=ACT.Sigmoid)
        make_identity(nc, ident[:])

        h_view = h_relu.rearrange("b (p t) y x -> p b t (y x)", t=PACK)
        p_view = prototypes.rearrange("(k r) d -> r k d", r=P)

        def load_group(g):
            images = slice(g * GROUP_IMAGES, (g + 1) * GROUP_IMAGES)
            nc.sync.dma_start(out=h_raw[:, images], in_=h_view[:, images])

        nc.scalar.dma_start(
            out=bias_rows[0 : CHANNELS // (PAIR * P), :].bitcast(BF16),
            in_=conv2_b.rearrange("(u i) -> u i", i=PAIR * P),
        )
        for b in range(0, 2):
            nc.sync.dma_start(out=h_raw[:, b], in_=h_view[:, b])
        scale_rows = conv2_w_scales.rearrange("g q n -> (g q) n")
        for quadrant in range(4):
            nc.sync.dma_start(
                out=w_scales_raw[32 * quadrant : 32 * quadrant + 4, :].bitcast(I32),
                in_=scale_rows[4 * quadrant : 4 * quadrant + 4, :].bitcast(I32),
            )
        for b in range(2, GROUP_IMAGES):
            nc.sync.dma_start(out=h_raw[:, b], in_=h_view[:, b])
        nc.sync.dma_start(
            out=w_codes_raw[:].bitcast(I32), in_=conv2_w_words.rearrange("g p n t -> (g p) (n t)").bitcast(I32)
        )
        for c in range(PROTO_CHUNKS):
            tiles = slice(c * TILES_PER_CHUNK, (c + 1) * TILES_PER_CHUNK)
            nc.sync.dma_start(out=p_raw[:, tiles, :], in_=p_view[:, tiles, :])
        for g in range(1, GROUPS):
            load_group(g)

        def warm_up(products):
            unread = scalar_psum.tile([P, BANK], F32, tag="s")
            for i in range(products):
                nc.tensor.matmul(out=unread[:], lhsT=zeros[:, 0:P], rhs=zeros[:], start=True, stop=True)

        def flip_bias():
            flipped = vector_psum.tile([P, P], F32, tag="v")
            nc.tensor.transpose(out=flipped[:], in_=bias_rows[:], identity=ident[:])
            nc.vector.tensor_copy(out=bias[:], in_=flipped[:, 0 : PACK // PAIR].bitcast(BF16))

        def order_w_codes():
            nc.vector.tensor_copy(
                out=w_codes[:].bitcast(I32).rearrange("p (u e m) -> p u e m", u=2, e=PAIR),
                in_=w_codes_raw[:].bitcast(I32).rearrange("p (u m e) -> p u e m", u=2, e=PAIR),
            )

        def order_w_scales():
            nc.vector.tensor_copy(
                out=w_scales[:].rearrange("p (u e m) -> p u e m", u=2, e=PAIR),
                in_=w_scales_raw[:].rearrange("p (u m e) -> p u e m", u=2, e=PAIR),
            )

        h_grouped_of = {}
        p_grouped_of = {}
        feat_of = {}
        f_grouped_of = {}
        f_codes_of = {}
        f_scales_of = {}
        f2_of = {}
        running_min_of = {}
        f2_gap_of = {}

        def regroup(engine, dst, src, factor=1.0):
            engine.tensor_scalar(out=dst, in0=src, scalar1=factor, scalar2=0.0, op0=ALU.mult, op1=ALU.add)

        def new_h_grouped(q):
            h_grouped = stage.tile([P, BANK, PACK], BF16, align_bytes=64, bufs=1)
            h_grouped_of[q] = h_grouped

        def group_first_h(images):
            if 0 not in h_grouped_of:
                new_h_grouped(0)
            by_image = h_grouped_of[0][:].rearrange("p (j b r) t -> p b j r t", b=GROUP_IMAGES, r=RUN)
            for b in images:
                regroup(nc.vector, by_image[:, b], h_raw[:, b, :, 0:P].rearrange("p t (j r) -> p j r t", r=RUN))

        def group_h(q, engine=nc.gpsimd):
            new_h_grouped(q)
            g = q // CHUNKS_PER_GROUP
            images = slice(g * GROUP_IMAGES, (g + 1) * GROUP_IMAGES)
            for j in range(TILES_PER_CHUNK):
                tile_in_group = (q % CHUNKS_PER_GROUP) * TILES_PER_CHUNK + j
                run = slice(tile_in_group * RUN, (tile_in_group + 1) * RUN)
                regroup(
                    engine,
                    h_grouped_of[q][:, j * P : (j + 1) * P, :].rearrange("p (b r) t -> p b r t", r=RUN),
                    h_raw[:, images, :, run].rearrange("p b t r -> p b r t"),
                )

        def quantise_h(q):
            nc.vector.quantize_mx(
                out=h_codes[:, q, :].bitcast(FP8X4),
                scales=h_scales[:, q, :],
                in_=h_grouped_of[q][:].rearrange("p c t -> p (c t)"),
            )

        def flip_prototypes(c, pair, on_scalar):
            if c not in p_grouped_of:
                p_grouped = stage.tile([P, BANK, PACK], BF16, align_bytes=64, bufs=PROTO_CHUNKS)
                p_grouped_of[c] = p_grouped
            if on_scalar:
                flipped = scalar_psum.tile([P, FLIPS, 2, P], F32, tag="s")
            else:
                flipped = vector_psum.tile([P, FLIPS, 2, P], F32, tag="v")
            for i in range(FLIPS):
                k = c * TILES_PER_CHUNK + pair * FLIPS + i
                words = p_raw[:, k, :].bitcast(F32)
                for u in range(2):
                    nc.tensor.transpose(out=flipped[:, i, u, :], in_=words[:, u * P : (u + 1) * P], identity=ident[:])
            rows = p_grouped_of[c][:, pair * FLIPS * P : (pair + 1) * FLIPS * P, :]
            dst = rows.rearrange("p r t -> p (r t)").bitcast(F32).rearrange("p (i r u) -> p i r u", u=2, r=P)
            src = flipped[:].rearrange("p i u r -> p i r u")
            if on_scalar:
                nc.scalar.copy(out=dst, in_=src)
            else:
                nc.vector.tensor_copy(out=dst, in_=src)

        def quantise_prototypes(c):
            nc.vector.quantize_mx(
                out=p_codes[:, c, :].bitcast(FP8X4),
                scales=p_scales[:, c, :],
                in_=p_grouped_of[c][:].rearrange("p c t -> p (c t)"),
            )

        def prototype_norm(k):
            squares = stage.tile([P, CHANNELS], BF16, tag="squares")
            nc.scalar.activation(out=squares[:], in_=p_raw[:, k, :], func=ACT.Square, accum_out=p2[:, k : k + 1])

        def conv_pass(q, t, out_columns, columns):
            nc.tensor.matmul_mx(
                out=out_columns,
                lhsT=w_codes[:, t * P : (t + 1) * P].bitcast(FP8X4),
                lhsT_scale=w_scales[:, t * P : (t + 1) * P],
                rhs=h_codes[:, q, columns].bitcast(FP8X4),
                rhs_scale=h_scales[:, q, columns],
                start=True,
                stop=True,
            )

        def sigmoid(q, t, columns, z):
            nc.scalar.activation(
                out=feat_of[q][:, t, columns], in_=z, func=ACT.Sigmoid, bias=bias[:, t : t + 1], scale=1.0
            )

        def conv(q):
            feat = stage.tile([P, PACK, BANK], F32)
            feat_of[q] = feat
            for t in range(PACK):
                z = scalar_psum.tile([P, BANK], F32, tag="s")
                conv_pass(q, t, z[:], slice(0, BANK))
                sigmoid(q, t, slice(0, BANK), z[:])

        def conv_half(q, half):
            if half == 0:
                feat = stage.tile([P, PACK, BANK], F32)
                feat_of[q] = feat
            columns = slice(half * HALF, (half + 1) * HALF)
            for u in range(2):
                z = scalar_psum.tile([P, PAIR, HALF], F32, tag="s")
                for e in range(PAIR):
                    conv_pass(q, PAIR * u + e, z[:, e, :], columns)
                for e in range(PAIR):
                    sigmoid(q, PAIR * u + e, columns, z[:, e, :])

        def group_f(q, columns=slice(0, BANK), factor=-2.0, engine=nc.gpsimd):
            if q not in f_grouped_of:
                f_grouped = stage.tile([P, BANK, PACK], BF16, align_bytes=64)
                f_grouped_of[q] = f_grouped
            regroup(
                engine,
                f_grouped_of[q][:, columns, :],
                feat_of[q][:, :, columns].rearrange("p t c -> p c t"),
                factor=factor,
            )

        def group_paired_f(q):
            group_f(q, slice(0, P), 2.0)
            group_f(q, slice(P, BANK))

        def quantise_f(q, columns=slice(0, BANK)):
            if q not in f_codes_of:
                f_codes = stage.tile([P, BANK], U32, align_bytes=64, bufs=3)
                f_scales = stage.tile([P, BANK], U8, align_bytes=64, bufs=3)
                f_codes_of[q] = f_codes
                f_scales_of[q] = f_scales
            nc.vector.quantize_mx(
                out=f_codes_of[q][:, columns].bitcast(FP8X4),
                scales=f_scales_of[q][:, columns],
                in_=f_grouped_of[q][:, columns, :].rearrange("p c t -> p (c t)"),
            )

        def feature_norms(q, tiles):
            if q not in f2_of:
                f2 = stage.tile([P, TILES_PER_CHUNK], F32, bufs=3)
                f2_of[q] = f2
            for j in tiles:
                flipped = scalar_psum.tile([P, PACK, P], F32, tag="s")
                for t in range(PACK):
                    nc.tensor.transpose(out=flipped[:, t, :], in_=feat_of[q][:, t, j * P : (j + 1) * P], identity=ident[:])
                squares = stage.tile([P, CHANNELS], BF16, tag="squares")
                nc.scalar.activation(
                    out=squares[:],
                    in_=flipped[:].rearrange("p t d -> p (t d)"),
                    func=ACT.Square,
                    accum_out=f2_of[q][:, j : j + 1],
                )

        def product(q, j, c, fp, start=True, stop=True):
            nc.tensor.matmul_mx(
                out=fp[:],
                lhsT=f_codes_of[q][:, j * P : (j + 1) * P].bitcast(FP8X4),
                lhsT_scale=f_scales_of[q][:, j * P : (j + 1) * P],
                rhs=p_codes[:, c, :].bitcast(FP8X4),
                rhs_scale=p_scales[:, c, :],
                start=start,
                stop=stop,
            )

        def begin_pair(q):
            f2_gap = stage.tile([P, 1], F32)
            f2_gap_of[q] = f2_gap
            f2 = f2_of[q]
            nc.scalar.activation(out=f2_gap[:], in_=f2[:, 0:1], func=ACT.Identity, bias=f2[:, 1:2], scale=-1.0)

        def pair_minimum(q, c, kept):
            fp = scalar_psum.tile([P, BANK], F32, tag="s")
            product(q, 1, c, fp)
            nc.scalar.activation(out=kept, in_=fp[:], func=ACT.Identity, bias=f2_of[q][:, 1:2], scale=1.0)
            gap = scalar_psum.tile([P, BANK], F32, tag="s")
            product(q, 1, c, gap, stop=False)
            product(q, 0, c, gap, start=False)
            excess = stage.tile([P, BANK], F32, bufs=4)
            nc.scalar.activation(out=excess[:], in_=gap[:], func=ACT.Relu, bias=f2_gap_of[q][:], scale=1.0)
            nc.gpsimd.tensor_tensor(out=kept, in0=kept, in1=excess[:], op=ALU.subtract)

        def split_minimum(q, c, kept):
            fp = scalar_psum.tile([P, BANK], F32, tag="s")
            product(q, 0, c, fp)
            nc.scalar.activation(out=kept, in_=fp[:], func=ACT.Identity, bias=f2_of[q][:, 0:1], scale=-1.0)
            other = vector_psum.tile([P, BANK], F32, tag="v")
            product(q, 1, c, other)
            nc.vector.scalar_tensor_tensor(
                out=kept, in0=other[:], scalar=f2_of[q][:, 1:2], in1=kept, op0=ALU.add, op1=ALU.min
            )

        def bank(tile, c):
            return tile[:, c * BANK : (c + 1) * BANK]

        def distances(q, j, chunks=range(PROTO_CHUNKS)):
            g = q // CHUNKS_PER_GROUP
            first_of_group = q % CHUNKS_PER_GROUP == 0 and j == 0
            if g not in running_min_of:
                running_min = stage.tile([P, PROTOS], F32)
                running_min_of[g] = running_min
            f2_column = f2_of[q][:, j : j + 1]
            for c in chunks:
                if first_of_group:
                    fp = scalar_psum.tile([P, BANK], F32, tag="s")
                else:
                    fp = vector_psum.tile([P, BANK], F32, tag="v")
                product(q, j, c, fp)
                kept = running_min_of[g][:, c * BANK : (c + 1) * BANK]
                if first_of_group:
                    nc.scalar.activation(out=kept, in_=fp[:], func=ACT.Identity, bias=f2_column, scale=1.0)
                else:
                    nc.vector.scalar_tensor_tensor(
                        out=kept, in0=fp[:], scalar=f2_column, in1=kept, op0=ALU.add, op1=ALU.min
                    )

        def fold_group(g, chunks=range(PROTO_CHUNKS)):
            images = slice(g * GROUP_IMAGES, (g + 1) * GROUP_IMAGES)
            for c in chunks:
                flipped = vector_psum.tile([P, TILES_PER_CHUNK, P], F32, tag="v")
                for i in range(TILES_PER_CHUNK):
                    k = c * TILES_PER_CHUNK + i
                    nc.tensor.transpose(
                        out=flipped[:, i, :], in_=running_min_of[g][:, k * P : (k + 1) * P], identity=ident[:]
                    )
                tiles = slice(c * TILES_PER_CHUNK, (c + 1) * TILES_PER_CHUNK)
                nc.vector.tensor_reduce(
                    out=best[:, images, tiles].rearrange("p b k -> p k b"),
                    in_=flipped[:].rearrange("p k (b r) -> p k b r", r=RUN),
                    op=ALU.min,
                    axis=AXIS.X,
                )

        result_of = {}
        rows_of = {}

        def add_p2(s):
            result = stage.tile([P, HALF_IMAGES, PROTO_TILES], F32)
            result_of[s] = result
            nc.vector.tensor_tensor(
                out=result[:],
                in0=best[:, s * HALF_IMAGES : (s + 1) * HALF_IMAGES, :],
                in1=p2[:].unsqueeze(1).to_broadcast([P, HALF_IMAGES, PROTO_TILES]),
                op=ALU.add,
            )

        def flip_result(s):
            rows = vector_psum.tile([P, P], F32, tag="v")
            rows_of[s] = rows
            nc.tensor.transpose(out=rows[:], in_=result_of[s][:].rearrange("p b k -> p (b k)"), identity=ident[:])

        def store_result(s):
            result_rows = stage.tile([P, P], F32)
            nc.vector.tensor_copy(out=result_rows[:], in_=rows_of[s][:])
            images = slice(s * HALF_IMAGES, (s + 1) * HALF_IMAGES)
            nc.sync.dma_start(out=out[images, :].rearrange("b (k r) -> (b k) r", r=P), in_=result_rows[:])

        first, second = slice(0, HALF), slice(HALF, BANK)
        group_first_h((0, 1))
        order_w_scales()
        group_first_h((2, 3))
        warm_up(6)
        flip_bias()
        warm_up(10)
        quantise_h(0)
        order_w_codes()
        group_h(1, nc.vector)
        conv_half(0, 0)
        flip_prototypes(0, 0, False)
        flip_prototypes(0, 1, False)
        conv_half(0, 1)
        group_f(0, first, engine=nc.vector)
        warm_up(2)
        quantise_f(0, first)
        quantise_prototypes(0)
        flip_prototypes(1, 0, False)
        feature_norms(0, (1, 0))
        group_f(0, second, engine=nc.vector)
        flip_prototypes(1, 1, False)
        warm_up(2)
        flip_prototypes(2, 0, True)
        flip_prototypes(2, 1, True)
        quantise_f(0, second)
        distances(0, 0, (0,))
        quantise_prototypes(1)
        distances(0, 1, (0,))
        feature_norms(0, (3, 2))
        flip_prototypes(3, 0, True)
        flip_prototypes(3, 1, True)
        quantise_h(1)
        quantise_prototypes(2)
        group_h(2)
        distances(0, 2, (0,))
        distances(0, 3, (0,))
        distances(0, 0, (1,))
        distances(0, 1, (1,))
        distances(0, 0, (2,))
        distances(0, 2, (1,))
        distances(0, 3, (1,))
        conv(1)
        group_f(1)
        quantise_prototypes(3)
        distances(0, 1, (2,))
        distances(0, 2, (2,))
        distances(0, 3, (2,))
        distances(0, 0, (3,))
        feature_norms(1, (0, 1))
        distances(0, 1, (3,))
        distances(0, 2, (3,))
        feature_norms(1, (2, 3))
        quantise_f(1)
        quantise_h(2)
        distances(0, 3, (3,))

        last = CHUNKS - 1
        norms = 0
        for q in range(1, last):
            if q % CHUNKS_PER_GROUP == 0:
                fold_group(q // CHUNKS_PER_GROUP - 1)
            else:
                distances(q, 0)
            if q + 1 < last:
                group_h(q + 2)
            conv(q + 1)
            if q + 1 < last:
                group_f(q + 1)
            else:
                group_paired_f(last)
            distances(q, 1)
            for k in range(norms, norms + (4 if q % CHUNKS_PER_GROUP else 2)):
                if k < PROTO_TILES:
                    prototype_norm(k)
            norms += 4 if q % CHUNKS_PER_GROUP else 2
            distances(q, 2)
            feature_norms(q + 1, (0, 1))
            distances(q, 3, (0,))
            quantise_f(q + 1)
            if q + 1 < last:
                quantise_h(q + 2)
            else:
                add_p2(0)
            feature_norms(q + 1, (2, 3))
            distances(q, 3, (1, 2, 3))
            if (q + 1) % CHUNKS_PER_GROUP == 0:
                distances(q + 1, 0, range(PROTO_CHUNKS - 1, -1, -1))

        begin_pair(last)
        paired = keep.tile([P, PROTOS], F32)
        kept = running_min_of[GROUPS - 1]
        for c in range(PROTO_CHUNKS):
            if c + 1 < PROTO_CHUNKS:
                pair_minimum(last, c, bank(paired, c))
            distances(last, 2, (c,))
            distances(last, 3, (c,))
        split_minimum(last, PROTO_CHUNKS - 1, bank(paired, PROTO_CHUNKS - 1))
        flip_result(0)
        for c in range(PROTO_CHUNKS):
            nc.vector.tensor_tensor(out=bank(kept, c), in0=bank(kept, c), in1=bank(paired, c), op=ALU.min)
        fold_group(GROUPS - 1)
        add_p2(1)
        flip_result(1)
        store_result(0)
        store_result(1)
